import numpy as np
import ml_dtypes


def mxq(x, axis, fmt="e4m3"):
    dtype, down = {"e4m3": (ml_dtypes.float8_e4m3fn, 7), "e5m2": (ml_dtypes.float8_e5m2, 14)}[fmt]
    v = np.moveaxis(np.asarray(x, np.float32).astype(ml_dtypes.bfloat16).astype(np.float64), axis, -1)
    blocks = v.reshape(v.shape[:-1] + (-1, 32))
    amax = np.abs(blocks).max(-1, keepdims=True)
    byte = np.maximum(np.where(amax > 0, np.frexp(amax)[1] - 1 + 127, 0) - down, 1)
    scale = np.exp2(byte - 127.0)
    codes = (blocks / scale).astype(np.float32).astype(dtype).astype(np.float64)
    return np.moveaxis((codes * scale).reshape(v.shape), -1, axis)


WIDE = False


def mx_kscale(k):
    if not WIDE:
        return np.ones(k)
    levels = np.array([10, -10, 5, -5, 0])
    if k % 512:
        return np.exp2(np.random.permutation(np.resize(levels, k // 32))).repeat(32)
    a = np.empty((k // 512, 16))
    for p in range(k // 512):
        a[p, :8] = np.random.permutation(np.resize(levels, 8))
        for g in range(8):
            far = levels[np.abs(levels - a[p, g]) >= 10]
            a[p, g + 8] = far[np.random.randint(len(far))]
    return np.exp2(a.ravel()).repeat(32)


BF16 = ml_dtypes.bfloat16


def bf(x):
    return np.asarray(x, np.float32).astype(BF16)


def f64(x):
    return np.asarray(x).astype(np.float64)


B, S, K, IN, HID, OUT = 4, 128, 16, 1024, 512, 127
LN_EPS = 1e-5
LINK_EPS = 1e-8


def sigmoid(v):
    return 1.0 / (1.0 + np.exp(-v))


def setup_inputs():
    s, t = mx_kscale(IN), mx_kscale(HID)
    keep = np.random.random((B, S, 1, 1)) > 0.125
    return {"net_in": bf(np.random.standard_normal((B, S, K, IN)) * s),
            "embeds": bf(np.random.standard_normal((B, S, OUT)) * 0.5),
            "m": bf(np.random.random((B, S, K, 1)) * keep),
            "W1": bf(np.random.standard_normal((IN, HID)) / np.sqrt(IN) / s[:, None] * t),
            "b1": bf(np.random.standard_normal(HID) * 0.3 * t),
            "Wf": bf(np.random.standard_normal((HID, OUT + 1)) * 3.0 / np.sqrt(HID) / t[:, None]),
            "b_f": bf(np.random.standard_normal(OUT + 1) * 0.3),
            "gamma": bf(1.0 + 0.1 * np.random.standard_normal(OUT)),
            "beta": bf(0.1 * np.random.standard_normal(OUT))}


def reference(net_in, embeds, m, W1, b1, Wf, b_f, gamma, beta):
    h = np.maximum((mxq(f64(net_in), 3, "e4m3") @ mxq(f64(W1), 0, "e4m3")) + f64(b1), 0.0)
    out = (mxq(h, 3, "e4m3") @ mxq(f64(Wf), 0, "e4m3")) + f64(b_f)
    out = np.concatenate([out[..., :-1], sigmoid(out[..., -1:])], axis=-1)
    out = f64(m) * out
    link_weight = out[..., -1] + LINK_EPS
    norm = link_weight.sum(axis=2, keepdims=True)
    weights = (link_weight / norm)[..., None]
    updates = (out * weights).sum(axis=2)
    upd_weights = updates[..., -1:]
    embeds_new = f64(embeds) + upd_weights * updates[..., :-1]
    mu = embeds_new.mean(axis=-1, keepdims=True)
    var = ((embeds_new - mu) ** 2).mean(axis=-1, keepdims=True)
    return (embeds_new - mu) / np.sqrt(var + LN_EPS) * f64(gamma) + f64(beta)

@@ -1,0 +1,354 @@
+from contextlib import ExitStack
+
+import concourse.mybir as mybir
+from concourse.masks import make_identity
+
+F32 = mybir.dt.float32
+BF16 = mybir.dt.bfloat16
+U32 = mybir.dt.uint32
+U8 = mybir.dt.uint8
+FP8X4 = mybir.dt.float8_e4m3fn_x4
+ALU = mybir.AluOpType
+ACT = mybir.ActivationFunctionType
+AX = mybir.AxisListType
+
+P = 128
+B, S, K, IN, HID, OUT = 4, 128, 16, 1024, 512, 127
+CH = OUT + 1
+LPC = 4
+NCH = B * K // LPC
+ROWS = LPC * P
+LN_EPS = 1e-5
+LINK_EPS = 1e-8
+
+FLOPS = 2 * B * S * K * IN * HID + 2 * B * S * K * HID * CH
+
+UNIT_LAG = 2
+M2_LAG = 2
+S_REGROUP_FROM = 3
+PIECES = tuple((c, 0, LPC) for c in range(NCH - 1)) + ((NCH - 1, 0, 2), (NCH - 1, 2, 1), (NCH - 1, 3, 1))
+NP = len(PIECES)
+
+
+def tile_embed_update_pa_t_kernel(tc, net_in, embeds, m, W1, b1, Wf, b_f, gamma, beta, out):
+    nc = tc.nc
+    with ExitStack() as ctx:
+        const = ctx.enter_context(tc.tile_pool(name="const", bufs=1))
+        xpool = ctx.enter_context(tc.tile_pool(name="xpool", bufs=5))
+        gpool = ctx.enter_context(tc.tile_pool(name="gpool", bufs=3))
+        net = ctx.enter_context(tc.tile_pool(name="net", bufs=14))
+        work = ctx.enter_context(tc.tile_pool(name="work", bufs=3))
+        small = ctx.enter_context(tc.tile_pool(name="small", bufs=2))
+        psum = ctx.enter_context(tc.psum_pool(name="psum", bufs=8))
+
+        junk = const.tile([P, 1], F32)
+        nc.vector.memset(junk[:], 0.0)
+        nc.scalar.activation(out=junk[:], in_=junk[:], func=ACT.Sigmoid)
+
+        xin = {}
+
+        def load(c):
+            b, kq = divmod(c, K // LPC)
+            xt_in = xpool.tile([P, LPC * IN], BF16, name="xin")
+            cuts = 2 if c == 0 else 1
+            width = LPC * IN // cuts
+            for h in range(cuts):
+                nc.sync.dma_start(
+                    out=xt_in[:, h * width:(h + 1) * width],
+                    in_=net_in[b].rearrange("s k i -> s (k i)")[:, kq * LPC * IN + h * width:kq * LPC * IN + (h + 1) * width],
+                )
+            xin[c] = xt_in
+
+        load(0)
+        w1raw = const.tile([P, 8, HID], BF16)
+        nc.sync.dma_start(
+            out=w1raw[:].rearrange("p (g j) h -> p g (j h)", j=4),
+            in_=W1.rearrange("(g p j) h -> p g (j h)", g=2, p=P, j=4),
+        )
+        b1raw = const.tile([P, 4], BF16)
+        nc.scalar.dma_start(out=b1raw[:], in_=b1.rearrange("(q t) -> q t", t=4))
+        wfraw = const.tile([P, 4, CH], BF16)
+        nc.scalar.dma_start(out=wfraw[:].rearrange("p t c -> p (t c)"), in_=Wf.rearrange("(q t) c -> q (t c)", t=4))
+        rows3 = const.tile([P, 4, CH], BF16)
+        nc.vector.memset(rows3[:], 0.0)
+        nc.scalar.dma_start(out=rows3[0:1, 0, :], in_=b_f.unsqueeze(0))
+        nc.scalar.dma_start(out=rows3[0:1, 1, 0:OUT], in_=gamma.unsqueeze(0))
+        nc.scalar.dma_start(out=rows3[0:1, 2, 0:OUT], in_=beta.unsqueeze(0))
+        msb = const.tile([P, B, K], BF16)
+        nc.scalar.dma_start(out=msb[:], in_=m.rearrange("b s k o -> s b (k o)"))
+        emb = const.tile([P, B, CH], BF16)
+        nc.scalar.dma_start(out=emb[:, :, 0:OUT], in_=embeds.rearrange("b s c -> s b c"))
+        for c in range(1, NCH):
+            load(c)
+
+        ident = const.tile([P, P], F32)
+        make_identity(nc, ident[:])
+        neghalf = const.tile([P, 1], F32)
+        nc.vector.memset(neghalf[:], -0.5)
+        ones = const.tile([P, P], BF16)
+        nc.vector.memset(ones[:], 1.0)
+        spread = const.tile([P, 3, CH], F32)
+        eps_ln = const.tile([P, 1], F32)
+        nc.vector.memset(eps_ln[:], LN_EPS)
+
+        def spread_rows():
+            spread_ps = psum.tile([P, 4, CH], F32, name="spread_ps", tag="bank")
+            nc.tensor.matmul(out=spread_ps[:], lhsT=ones[:], rhs=rows3[:], start=True, stop=True)
+            nc.vector.tensor_copy(out=spread[:], in_=spread_ps[:, 0:3, :])
+            nc.vector.tensor_copy(out=bf127[:], in_=bfb[:, OUT:CH])
+
+        bfb = spread[:, 0, :]
+        gmb = spread[:, 1, :]
+        btb = spread[:, 2, :]
+
+        w1g = const.tile([P, 2, HID, 4], BF16, align_bytes=64)
+        w1c = const.tile([P, 2, HID], U32, align_bytes=64)
+        w1s = const.tile([P, 2, HID], U8, align_bytes=64)
+        b1f = const.tile([P, 4], F32)
+        wfg = const.tile([P, CH, 4], BF16, align_bytes=64)
+        bf127 = const.tile([P, 1], F32)
+        mf = const.tile([P, B * K], F32)
+        wfc = const.tile([P, CH], U32, align_bytes=64)
+        wfs = const.tile([P, CH], U8, align_bytes=64)
+
+        def quantise_w1(g):
+            nc.vector.quantize_mx(
+                out=w1c[:, g, :].bitcast(FP8X4),
+                scales=w1s[:, g, :],
+                in_=w1g[:, g].rearrange("p h j -> p (h j)"),
+            )
+
+        def prepare_weights():
+            for g in range(2):
+                src = w1raw[:, 4 * g:4 * g + 4, :].rearrange("p j (q t) -> p t q j", t=4)
+                dst = w1g[:, g].rearrange("p (t q) j -> p t q j", t=4)
+                if g == 0:
+                    nc.vector.tensor_copy(out=dst, in_=src)
+                else:
+                    nc.scalar.copy(out=dst, in_=src)
+            nc.vector.tensor_copy(out=b1f[:], in_=b1raw[:])
+            quantise_w1(0)
+            nc.vector.tensor_copy(out=wfg[:], in_=wfraw[:].rearrange("p t c -> p c t"))
+            nc.vector.tensor_copy(out=mf[:], in_=msb[:].rearrange("p b k -> p (b k)"))
+            nc.vector.quantize_mx(out=wfc[:].bitcast(FP8X4), scales=wfs[:], in_=wfg[:].rearrange("p c t -> p (c t)"))
+            quantise_w1(1)
+
+        sig = const.tile([P, B * K], F32)
+        gall = const.tile([P, B * K], F32)
+        sums_in = const.tile([P, B, 3, K], F32)
+
+        gnet, ncod, nsca, hpl, hgr, hcod, hsca, opb, acc = {}, {}, {}, {}, {}, {}, {}, {}, {}
+
+        def stage_a(c, banks):
+            xf = xin[c][:].bitcast(F32)
+            if c not in gnet:
+                gn_new = gpool.tile([P, 2, ROWS, 2], F32, name="gnet", align_bytes=64)
+                gnet[c] = gn_new
+            gn = gnet[c]
+            for j in banks:
+                lp, g = divmod(j, 2)
+                xt = psum.tile([P, 2, 2 * P], F32, name="xt", tag="bank")
+                for u in range(2):
+                    for li in range(2):
+                        col = (2 * lp + li) * (IN // 2) + g * 256
+                        nc.tensor.transpose(xt[:, u, li * P:(li + 1) * P], xf[:, col + u:col + 2 * P:2], ident[:])
+                dst = gn[:, g, lp * 2 * P:(lp + 1) * 2 * P, :]
+                src = xt[:].rearrange("p u r -> p r u")
+                if j == 3:
+                    nc.vector.tensor_copy(out=dst, in_=src)
+                else:
+                    nc.scalar.copy(out=dst, in_=src)
+
+        def stage_b(c):
+            nco = net.tile([P, 2, ROWS], U32, name="ncod", align_bytes=64)
+            nsc = net.tile([P, 2, ROWS], U8, name="nsca", align_bytes=64)
+            ncod[c], nsca[c] = nco, nsc
+            nc.vector.quantize_mx(
+                out=nco[:].rearrange("p g r -> p (g r)").bitcast(FP8X4),
+                scales=nsc[:].rearrange("p g r -> p (g r)"),
+                in_=gnet[c][:].rearrange("p g r u -> p (g r u)").bitcast(BF16),
+            )
+
+        def stage_c(n, t):
+            c, l0, nl = PIECES[n]
+            if n not in hpl:
+                hp_new = work.tile([P, 4, ROWS], BF16, name="hpl")
+                hpl[n] = hp_new
+            rows = slice(l0 * P, (l0 + nl) * P)
+            hp = psum.tile([P, ROWS], F32, name="hp", tag="bank")
+            for g in range(2):
+                nc.tensor.matmul_mx(
+                    out=hp[:, 0:nl * P],
+                    lhsT=w1c[:, g, t * P:(t + 1) * P].bitcast(FP8X4),
+                    lhsT_scale=w1s[:, g, t * P:(t + 1) * P],
+                    rhs=ncod[c][:, g, rows].bitcast(FP8X4),
+                    rhs_scale=nsca[c][:, g, rows],
+                    start=(g == 0),
+                    stop=(g == 1),
+                )
+            nc.scalar.activation(out=hpl[n][:, t, 0:nl * P], in_=hp[:, 0:nl * P], func=ACT.Relu,
+                                 bias=b1f[:, t:t + 1], scale=1.0)
+
+        def regroup(copy, n, r0, r1):
+            copy(
+                out=hgr[n][:, r0:r1, :].rearrange("p (c i) t -> p c t i", i=4),
+                in_=hpl[n][:, :, r0:r1].rearrange("p t (c i) -> p c t i", i=4),
+            )
+
+        def stage_d(n):
+            nl = PIECES[n][2]
+            hg = work.tile([P, ROWS, 4], BF16, name="hgr", align_bytes=64)
+            hgr[n] = hg
+            if nl == LPC and n >= S_REGROUP_FROM:
+                regroup(nc.vector.tensor_copy, n, 0, ROWS - P)
+                regroup(nc.scalar.copy, n, ROWS - P, ROWS)
+            else:
+                regroup(nc.vector.tensor_copy, n, 0, nl * P)
+
+        def stage_e(n):
+            nl = PIECES[n][2]
+            hco = work.tile([P, ROWS], U32, name="hcod", align_bytes=64)
+            hsc = work.tile([P, ROWS], U8, name="hsca", align_bytes=64)
+            hcod[n], hsca[n] = hco, hsc
+            nc.vector.quantize_mx(out=hco[:, 0:nl * P].bitcast(FP8X4), scales=hsc[:, 0:nl * P],
+                                  in_=hgr[n][:, 0:nl * P, :].rearrange("p r t -> p (r t)"))
+
+        def links(n):
+            c, l0, nl = PIECES[n]
+            return c * LPC + l0, nl
+
+        def stage_f(n):
+            first, nl = links(n)
+            op = psum.tile([P, LPC, CH], F32, name="op", tag="bank")
+            opb[n] = op
+            for l in range(nl):
+                nc.tensor.matmul_mx(
+                    out=op[:, l, :],
+                    lhsT=hcod[n][:, l * P:(l + 1) * P].bitcast(FP8X4),
+                    lhsT_scale=hsca[n][:, l * P:(l + 1) * P],
+                    rhs=wfc[:].bitcast(FP8X4),
+                    rhs_scale=wfs[:],
+                    start=True,
+                    stop=True,
+                )
+            nc.scalar.activation(out=sig[:, first:first + nl], in_=op[:, 0:nl, OUT], func=ACT.Sigmoid,
+                                 bias=bf127[:, 0:1], scale=1.0)
+            if n == NP - 1:
+                nc.scalar.activation(out=junk[:], in_=sig[:, first:first + 1], func=ACT.Abs_reciprocal_sqrt,
+                                     bias=eps_ln[:, 0:1], scale=1.0)
+
+        def stage_gq(n):
+            first, nl = links(n)
+            b, k0 = divmod(first, K)
+            cols = slice(first, first + nl)
+            nc.vector.tensor_tensor(out=gall[:, cols], in0=sig[:, cols], in1=mf[:, cols], op=ALU.mult)
+            nc.vector.scalar_tensor_tensor(out=sums_in[:, b, 2, k0:k0 + nl], in0=gall[:, cols], scalar=LINK_EPS,
+                                           in1=mf[:, cols], op0=ALU.add, op1=ALU.mult)
+
+        def stage_stt(n):
+            first, nl = links(n)
+            b, k0 = divmod(first, K)
+            op = opb[n]
+            if k0 == 0:
+                acc_b = small.tile([P, 2, CH], F32, name="acc")
+                acc[b] = acc_b
+            a = acc[b]
+            for l in range(nl):
+                k = k0 + l
+                qs = sums_in[:, b, 2, k:k + 1]
+                if k < 2:
+                    nc.vector.tensor_scalar(out=a[:, k % 2, :], in0=op[:, l, :], scalar1=qs, scalar2=None, op0=ALU.mult)
+                else:
+                    nc.vector.scalar_tensor_tensor(out=a[:, k % 2, :], in0=op[:, l, :], scalar=qs, in1=a[:, k % 2, :],
+                                                   op0=ALU.mult, op1=ALU.add)
+
+        ln_y1, ln_rstd = {}, {}
+
+        def stage_ln1(b):
+            g16 = gall[:, b * K:(b + 1) * K]
+            nc.vector.tensor_scalar_add(out=sums_in[:, b, 0, :], in0=g16, scalar1=LINK_EPS)
+            nc.vector.scalar_tensor_tensor(out=sums_in[:, b, 1, :], in0=g16, scalar=LINK_EPS, in1=g16,
+                                           op0=ALU.add, op1=ALU.mult)
+            sums = small.tile([P, 3], F32, name="sums")
+            nc.vector.tensor_reduce(out=sums[:], in_=sums_in[:, b], axis=AX.X, op=ALU.add)
+            rl = small.tile([P, 1], F32, name="rl")
+            nc.vector.reciprocal(out=rl[:], in_=sums[:, 0:1])
+            w0 = small.tile([P, OUT], F32, name="w0")
+            nc.vector.scalar_tensor_tensor(out=w0[:], in0=bfb[:, 0:OUT], scalar=sums[:, 2:3], in1=acc[b][:, 0, 0:OUT],
+                                           op0=ALU.mult, op1=ALU.add)
+            s1 = small.tile([P, 1], F32, name="s1")
+            nc.vector.tensor_scalar(out=s1[:], in0=sums[:, 1:2], scalar1=rl[:, 0:1], scalar2=rl[:, 0:1],
+                                    op0=ALU.mult, op1=ALU.mult)
+            w1 = small.tile([P, OUT], F32, name="w1")
+            nc.vector.tensor_tensor(out=w1[:], in0=w0[:], in1=acc[b][:, 1, 0:OUT], op=ALU.add)
+            e2 = small.tile([P, OUT], F32, name="e2")
+            nc.vector.scalar_tensor_tensor(out=e2[:], in0=w1[:], scalar=s1[:, 0:1], in1=emb[:, b, 0:OUT],
+                                           op0=ALU.mult, op1=ALU.add)
+            st6 = small.tile([P, 6], F32, name="st6")
+            nc.vector.bn_stats(out=st6[:], in_=e2[:])
+            mv = small.tile([P, 2], F32, name="mv")
+            nc.vector.bn_aggr(out=mv[:], in_=st6[:])
+            rstd = small.tile([P, 1], F32, name="rstd")
+            if b == B - 1:
+                nc.scalar.activation(out=rstd[:], in_=mv[:, 1:2], func=ACT.Abs_reciprocal_sqrt,
+                                     bias=eps_ln[:, 0:1], scale=1.0)
+            else:
+                vpe = small.tile([P, 1], F32, name="vpe")
+                nc.gpsimd.tensor_scalar_add(out=vpe[:], in0=mv[:, 1:2], scalar1=LN_EPS)
+                nc.gpsimd.tensor_tensor(out=rstd[:], in0=vpe[:], in1=neghalf[:], op=ALU.pow)
+            y1 = small.tile([P, OUT], F32, name="y1")
+            nc.vector.scalar_tensor_tensor(out=y1[:], in0=e2[:], scalar=mv[:, 0:1], in1=gmb[:, 0:OUT],
+                                           op0=ALU.subtract, op1=ALU.mult)
+            ln_y1[b], ln_rstd[b] = y1, rstd
+
+        def stage_ln2(b):
+            y2 = small.tile([P, OUT], F32, name="y2")
+            nc.vector.scalar_tensor_tensor(out=y2[:], in0=ln_y1[b][:], scalar=ln_rstd[b][:, 0:1], in1=btb[:, 0:OUT],
+                                           op0=ALU.mult, op1=ALU.add)
+            nc.sync.dma_start(out=out[b], in_=y2[:])
+
+        def on(n):
+            return 0 <= n < NP
+
+        def ends_batch(n):
+            first, nl = links(n)
+            return (first + nl) % K == 0
+
+        def piece_closed(n):
+            if on(n - M2_LAG):
+                stage_f(n - M2_LAG)
+            if on(n - 1):
+                stage_d(n - 1)
+            j = n - M2_LAG - 1
+            if on(j):
+                stage_gq(j)
+                stage_stt(j)
+            if on(j - 1) and ends_batch(j - 1):
+                stage_ln2(links(j - 1)[0] // K)
+            if on(j) and ends_batch(j):
+                stage_ln1(links(j)[0] // K)
+            if on(n - 1):
+                stage_e(n - 1)
+
+        def h_bank(i):
+            n, t = divmod(i, 4)
+            stage_c(n, t)
+            if t == 3:
+                piece_closed(n)
+
+        with tc.manual_schedule():
+            for c in range(NCH):
+                stage_a(c, (0, 1, 2, 3))
+                if c == 0:
+                    prepare_weights()
+                if c == 1:
+                    spread_rows()
+                if c >= 1:
+                    stage_b(c - 1)
+                if c >= UNIT_LAG:
+                    h_bank(c - UNIT_LAG)
+            stage_b(NCH - 1)
+        for i in range(NCH - UNIT_LAG, 4 * NP):
+            h_bank(i)
+        for n in range(NP, NP + M2_LAG + 2):
+            piece_closed(n)

@@ -23,27 +23,24 @@ LINK_EPS = 1e-8
 
 FLOPS = 2 * B * S * K * IN * HID + 2 * B * S * K * HID * CH
 
-UNIT_LAG = 2
-M2_LAG = 2
-S_REGROUP_FROM = 3
-PIECES = tuple((c, 0, LPC) for c in range(NCH - 1)) + ((NCH - 1, 0, 2), (NCH - 1, 2, 1), (NCH - 1, 3, 1))
+PIECES = tuple((c, 0, LPC) for c in range(NCH - 1)) + ((NCH - 1, 0, 2), (NCH - 1, 2, 2))
 NP = len(PIECES)
+LAST_FULL = NCH - 2
 
 
 def tile_embed_update_pa_t_kernel(tc, net_in, embeds, m, W1, b1, Wf, b_f, gamma, beta, out):
     nc = tc.nc
     with ExitStack() as ctx:
         const = ctx.enter_context(tc.tile_pool(name="const", bufs=1))
-        xpool = ctx.enter_context(tc.tile_pool(name="xpool", bufs=5))
+        xpool = ctx.enter_context(tc.tile_pool(name="xpool", bufs=6))
         gpool = ctx.enter_context(tc.tile_pool(name="gpool", bufs=3))
-        net = ctx.enter_context(tc.tile_pool(name="net", bufs=14))
+        net = ctx.enter_context(tc.tile_pool(name="net", bufs=3))
         work = ctx.enter_context(tc.tile_pool(name="work", bufs=3))
         small = ctx.enter_context(tc.tile_pool(name="small", bufs=2))
-        psum = ctx.enter_context(tc.psum_pool(name="psum", bufs=8))
-
-        junk = const.tile([P, 1], F32)
-        nc.vector.memset(junk[:], 0.0)
-        nc.scalar.activation(out=junk[:], in_=junk[:], func=ACT.Sigmoid)
+        tbanks = ctx.enter_context(tc.psum_pool(name="tbanks", bufs=4))
+        hbanks = ctx.enter_context(tc.psum_pool(name="hbanks", bufs=3))
+        obank = ctx.enter_context(tc.psum_pool(name="obank", bufs=1))
+        ctx.enter_context(tc.manual_schedule())
 
         xin = {}
 
@@ -59,12 +56,13 @@ def tile_embed_update_pa_t_kernel(tc, net_in, embeds, m, W1, b1, Wf, b_f, gamma,
                 )
             xin[c] = xt_in
 
-        load(0)
         w1raw = const.tile([P, 8, HID], BF16)
-        nc.sync.dma_start(
-            out=w1raw[:].rearrange("p (g j) h -> p g (j h)", j=4),
-            in_=W1.rearrange("(g p j) h -> p g (j h)", g=2, p=P, j=4),
-        )
+        for g in range(2):
+            nc.sync.dma_start(
+                out=w1raw[:, 4 * g:4 * g + 4, :].rearrange("p j h -> p (j h)"),
+                in_=W1[4 * P * g:4 * P * (g + 1), :].rearrange("(p j) h -> p (j h)", j=4),
+            )
+        load(0)
         b1raw = const.tile([P, 4], BF16)
         nc.scalar.dma_start(out=b1raw[:], in_=b1.rearrange("(q t) -> q t", t=4))
         wfraw = const.tile([P, 4, CH], BF16)
@@ -81,6 +79,10 @@ def tile_embed_update_pa_t_kernel(tc, net_in, embeds, m, W1, b1, Wf, b_f, gamma,
         for c in range(1, NCH):
             load(c)
 
+        junk = const.tile([P, 1], F32)
+        nc.vector.memset(junk[:], 0.0)
+        nc.scalar.activation(out=junk[:], in_=junk[:], func=ACT.Sigmoid)
+
         ident = const.tile([P, P], F32)
         make_identity(nc, ident[:])
         neghalf = const.tile([P, 1], F32)
@@ -92,7 +94,7 @@ def tile_embed_update_pa_t_kernel(tc, net_in, embeds, m, W1, b1, Wf, b_f, gamma,
         nc.vector.memset(eps_ln[:], LN_EPS)
 
         def spread_rows():
-            spread_ps = psum.tile([P, 4, CH], F32, name="spread_ps", tag="bank")
+            spread_ps = obank.tile([P, LPC, CH], F32, name="spread_ps", tag="bank")
             nc.tensor.matmul(out=spread_ps[:], lhsT=ones[:], rhs=rows3[:], start=True, stop=True)
             nc.vector.tensor_copy(out=spread[:], in_=spread_ps[:, 0:3, :])
             nc.vector.tensor_copy(out=bf127[:], in_=bfb[:, OUT:CH])
@@ -118,19 +120,21 @@ def tile_embed_update_pa_t_kernel(tc, net_in, embeds, m, W1, b1, Wf, b_f, gamma,
                 in_=w1g[:, g].rearrange("p h j -> p (h j)"),
             )
 
+        def regroup_w1(copy, g, t0, t1):
+            copy(
+                out=w1g[:, g].rearrange("p (t q) j -> p t q j", t=4)[:, t0:t1],
+                in_=w1raw[:, 4 * g:4 * g + 4, :].rearrange("p j (q t) -> p t q j", t=4)[:, t0:t1],
+            )
+
         def prepare_weights():
-            for g in range(2):
-                src = w1raw[:, 4 * g:4 * g + 4, :].rearrange("p j (q t) -> p t q j", t=4)
-                dst = w1g[:, g].rearrange("p (t q) j -> p t q j", t=4)
-                if g == 0:
-                    nc.vector.tensor_copy(out=dst, in_=src)
-                else:
-                    nc.scalar.copy(out=dst, in_=src)
-            nc.vector.tensor_copy(out=b1f[:], in_=b1raw[:])
-            quantise_w1(0)
+            regroup_w1(nc.vector.tensor_copy, 0, 0, 4)
+            regroup_w1(nc.scalar.copy, 1, 0, 2)
             nc.vector.tensor_copy(out=wfg[:], in_=wfraw[:].rearrange("p t c -> p c t"))
-            nc.vector.tensor_copy(out=mf[:], in_=msb[:].rearrange("p b k -> p (b k)"))
+            quantise_w1(0)
+            regroup_w1(nc.vector.tensor_copy, 1, 2, 4)
             nc.vector.quantize_mx(out=wfc[:].bitcast(FP8X4), scales=wfs[:], in_=wfg[:].rearrange("p c t -> p (c t)"))
+            nc.vector.tensor_copy(out=b1f[:], in_=b1raw[:])
+            nc.vector.tensor_copy(out=mf[:], in_=msb[:].rearrange("p b k -> p (b k)"))
             quantise_w1(1)
 
         sig = const.tile([P, B * K], F32)
@@ -139,25 +143,18 @@ def tile_embed_update_pa_t_kernel(tc, net_in, embeds, m, W1, b1, Wf, b_f, gamma,
 
         gnet, ncod, nsca, hpl, hgr, hcod, hsca, opb, acc = {}, {}, {}, {}, {}, {}, {}, {}, {}
 
-        def stage_a(c, banks):
+        def stage_a(c):
             xf = xin[c][:].bitcast(F32)
-            if c not in gnet:
-                gn_new = gpool.tile([P, 2, ROWS, 2], F32, name="gnet", align_bytes=64)
-                gnet[c] = gn_new
-            gn = gnet[c]
-            for j in banks:
+            gn = gpool.tile([P, 2, ROWS, 2], F32, name="gnet", align_bytes=64)
+            gnet[c] = gn
+            for j in range(4):
                 lp, g = divmod(j, 2)
-                xt = psum.tile([P, 2, 2 * P], F32, name="xt", tag="bank")
+                xt = tbanks.tile([P, 2, 2 * P], F32, name="xt", tag="bank")
                 for u in range(2):
                     for li in range(2):
                         col = (2 * lp + li) * (IN // 2) + g * 256
                         nc.tensor.transpose(xt[:, u, li * P:(li + 1) * P], xf[:, col + u:col + 2 * P:2], ident[:])
-                dst = gn[:, g, lp * 2 * P:(lp + 1) * 2 * P, :]
-                src = xt[:].rearrange("p u r -> p r u")
-                if j == 3:
-                    nc.vector.tensor_copy(out=dst, in_=src)
-                else:
-                    nc.scalar.copy(out=dst, in_=src)
+                nc.scalar.copy(out=gn[:, g, lp * 2 * P:(lp + 1) * 2 * P, :], in_=xt[:].rearrange("p u r -> p r u"))
 
         def stage_b(c):
             nco = net.tile([P, 2, ROWS], U32, name="ncod", align_bytes=64)
@@ -175,7 +172,7 @@ def tile_embed_update_pa_t_kernel(tc, net_in, embeds, m, W1, b1, Wf, b_f, gamma,
                 hp_new = work.tile([P, 4, ROWS], BF16, name="hpl")
                 hpl[n] = hp_new
             rows = slice(l0 * P, (l0 + nl) * P)
-            hp = psum.tile([P, ROWS], F32, name="hp", tag="bank")
+            hp = hbanks.tile([P, ROWS], F32, name="hp", tag="bank")
             for g in range(2):
                 nc.tensor.matmul_mx(
                     out=hp[:, 0:nl * P],
@@ -195,15 +192,10 @@ def tile_embed_update_pa_t_kernel(tc, net_in, embeds, m, W1, b1, Wf, b_f, gamma,
                 in_=hpl[n][:, :, r0:r1].rearrange("p t (c i) -> p c t i", i=4),
             )
 
-        def stage_d(n):
-            nl = PIECES[n][2]
+        def stage_d(n, copy):
             hg = work.tile([P, ROWS, 4], BF16, name="hgr", align_bytes=64)
             hgr[n] = hg
-            if nl == LPC and n >= S_REGROUP_FROM:
-                regroup(nc.vector.tensor_copy, n, 0, ROWS - P)
-                regroup(nc.scalar.copy, n, ROWS - P, ROWS)
-            else:
-                regroup(nc.vector.tensor_copy, n, 0, nl * P)
+            regroup(copy, n, 0, PIECES[n][2] * P)
 
         def stage_e(n):
             nl = PIECES[n][2]
@@ -219,7 +211,8 @@ def tile_embed_update_pa_t_kernel(tc, net_in, embeds, m, W1, b1, Wf, b_f, gamma,
 
         def stage_f(n):
             first, nl = links(n)
-            op = psum.tile([P, LPC, CH], F32, name="op", tag="bank")
+            pool = obank if n <= LAST_FULL else tbanks
+            op = pool.tile([P, LPC, CH], F32, name="op", tag="bank")
             opb[n] = op
             for l in range(nl):
                 nc.tensor.matmul_mx(
@@ -237,11 +230,15 @@ def tile_embed_update_pa_t_kernel(tc, net_in, embeds, m, W1, b1, Wf, b_f, gamma,
                 nc.scalar.activation(out=junk[:], in_=sig[:, first:first + 1], func=ACT.Abs_reciprocal_sqrt,
                                      bias=eps_ln[:, 0:1], scale=1.0)
 
-        def stage_gq(n):
+        def stage_g(n):
+            first, nl = links(n)
+            cols = slice(first, first + nl)
+            nc.vector.tensor_tensor(out=gall[:, cols], in0=sig[:, cols], in1=mf[:, cols], op=ALU.mult)
+
+        def stage_q(n):
             first, nl = links(n)
             b, k0 = divmod(first, K)
             cols = slice(first, first + nl)
-            nc.vector.tensor_tensor(out=gall[:, cols], in0=sig[:, cols], in1=mf[:, cols], op=ALU.mult)
             nc.vector.scalar_tensor_tensor(out=sums_in[:, b, 2, k0:k0 + nl], in0=gall[:, cols], scalar=LINK_EPS,
                                            in1=mf[:, cols], op0=ALU.add, op1=ALU.mult)
 
@@ -262,93 +259,120 @@ def tile_embed_update_pa_t_kernel(tc, net_in, embeds, m, W1, b1, Wf, b_f, gamma,
                     nc.vector.scalar_tensor_tensor(out=a[:, k % 2, :], in0=op[:, l, :], scalar=qs, in1=a[:, k % 2, :],
                                                    op0=ALU.mult, op1=ALU.add)
 
-        ln_y1, ln_rstd = {}, {}
+        woven = []
 
-        def stage_ln1(b):
+        def weave(count=1):
+            for op in woven[:count]:
+                op()
+            woven[:count] = []
+
+        def norm_ops(b):
             g16 = gall[:, b * K:(b + 1) * K]
-            nc.vector.tensor_scalar_add(out=sums_in[:, b, 0, :], in0=g16, scalar1=LINK_EPS)
-            nc.vector.scalar_tensor_tensor(out=sums_in[:, b, 1, :], in0=g16, scalar=LINK_EPS, in1=g16,
-                                           op0=ALU.add, op1=ALU.mult)
             sums = small.tile([P, 3], F32, name="sums")
-            nc.vector.tensor_reduce(out=sums[:], in_=sums_in[:, b], axis=AX.X, op=ALU.add)
             rl = small.tile([P, 1], F32, name="rl")
-            nc.vector.reciprocal(out=rl[:], in_=sums[:, 0:1])
-            w0 = small.tile([P, OUT], F32, name="w0")
-            nc.vector.scalar_tensor_tensor(out=w0[:], in0=bfb[:, 0:OUT], scalar=sums[:, 2:3], in1=acc[b][:, 0, 0:OUT],
-                                           op0=ALU.mult, op1=ALU.add)
             s1 = small.tile([P, 1], F32, name="s1")
-            nc.vector.tensor_scalar(out=s1[:], in0=sums[:, 1:2], scalar1=rl[:, 0:1], scalar2=rl[:, 0:1],
-                                    op0=ALU.mult, op1=ALU.mult)
+            w0 = small.tile([P, OUT], F32, name="w0")
             w1 = small.tile([P, OUT], F32, name="w1")
-            nc.vector.tensor_tensor(out=w1[:], in0=w0[:], in1=acc[b][:, 1, 0:OUT], op=ALU.add)
             e2 = small.tile([P, OUT], F32, name="e2")
-            nc.vector.scalar_tensor_tensor(out=e2[:], in0=w1[:], scalar=s1[:, 0:1], in1=emb[:, b, 0:OUT],
-                                           op0=ALU.mult, op1=ALU.add)
             st6 = small.tile([P, 6], F32, name="st6")
-            nc.vector.bn_stats(out=st6[:], in_=e2[:])
             mv = small.tile([P, 2], F32, name="mv")
-            nc.vector.bn_aggr(out=mv[:], in_=st6[:])
+            vpe = small.tile([P, 1], F32, name="vpe")
             rstd = small.tile([P, 1], F32, name="rstd")
-            if b == B - 1:
-                nc.scalar.activation(out=rstd[:], in_=mv[:, 1:2], func=ACT.Abs_reciprocal_sqrt,
-                                     bias=eps_ln[:, 0:1], scale=1.0)
-            else:
-                vpe = small.tile([P, 1], F32, name="vpe")
-                nc.gpsimd.tensor_scalar_add(out=vpe[:], in0=mv[:, 1:2], scalar1=LN_EPS)
-                nc.gpsimd.tensor_tensor(out=rstd[:], in0=vpe[:], in1=neghalf[:], op=ALU.pow)
             y1 = small.tile([P, OUT], F32, name="y1")
-            nc.vector.scalar_tensor_tensor(out=y1[:], in0=e2[:], scalar=mv[:, 0:1], in1=gmb[:, 0:OUT],
-                                           op0=ALU.subtract, op1=ALU.mult)
-            ln_y1[b], ln_rstd[b] = y1, rstd
-
-        def stage_ln2(b):
             y2 = small.tile([P, OUT], F32, name="y2")
-            nc.vector.scalar_tensor_tensor(out=y2[:], in0=ln_y1[b][:], scalar=ln_rstd[b][:, 0:1], in1=btb[:, 0:OUT],
-                                           op0=ALU.mult, op1=ALU.add)
-            nc.sync.dma_start(out=out[b], in_=y2[:])
+            a = acc[b]
 
-        def on(n):
-            return 0 <= n < NP
+            def variance():
+                nc.vector.bn_aggr(out=mv[:], in_=st6[:])
+                if b == B - 1:
+                    nc.scalar.activation(out=rstd[:], in_=mv[:, 1:2], func=ACT.Abs_reciprocal_sqrt,
+                                         bias=eps_ln[:, 0:1], scale=1.0)
+                else:
+                    nc.gpsimd.tensor_scalar_add(out=vpe[:], in0=mv[:, 1:2], scalar1=LN_EPS)
+                    nc.gpsimd.tensor_tensor(out=rstd[:], in0=vpe[:], in1=neghalf[:], op=ALU.pow)
+
+            def store():
+                nc.vector.scalar_tensor_tensor(out=y2[:], in0=y1[:], scalar=rstd[:, 0:1], in1=btb[:, 0:OUT],
+                                               op0=ALU.mult, op1=ALU.add)
+                nc.sync.dma_start(out=out[b], in_=y2[:])
+
+            return [
+                lambda: nc.vector.tensor_scalar_add(out=sums_in[:, b, 0, :], in0=g16, scalar1=LINK_EPS),
+                lambda: nc.vector.scalar_tensor_tensor(out=sums_in[:, b, 1, :], in0=g16, scalar=LINK_EPS, in1=g16,
+                                                       op0=ALU.add, op1=ALU.mult),
+                lambda: nc.vector.tensor_reduce(out=sums[:], in_=sums_in[:, b], axis=AX.X, op=ALU.add),
+                lambda: nc.vector.reciprocal(out=rl[:], in_=sums[:, 0:1]),
+                lambda: nc.vector.scalar_tensor_tensor(out=w0[:], in0=bfb[:, 0:OUT], scalar=sums[:, 2:3],
+                                                       in1=a[:, 0, 0:OUT], op0=ALU.mult, op1=ALU.add),
+                lambda: nc.vector.tensor_scalar(out=s1[:], in0=sums[:, 1:2], scalar1=rl[:, 0:1], scalar2=rl[:, 0:1],
+                                                op0=ALU.mult, op1=ALU.mult),
+                lambda: nc.vector.tensor_tensor(out=w1[:], in0=w0[:], in1=a[:, 1, 0:OUT], op=ALU.add),
+                lambda: nc.vector.scalar_tensor_tensor(out=e2[:], in0=w1[:], scalar=s1[:, 0:1], in1=emb[:, b, 0:OUT],
+                                                       op0=ALU.mult, op1=ALU.add),
+                lambda: nc.vector.bn_stats(out=st6[:], in_=e2[:]),
+                variance,
+                lambda: nc.vector.scalar_tensor_tensor(out=y1[:], in0=e2[:], scalar=mv[:, 0:1], in1=gmb[:, 0:OUT],
+                                                       op0=ALU.subtract, op1=ALU.mult),
+                store,
+            ]
 
         def ends_batch(n):
             first, nl = links(n)
             return (first + nl) % K == 0
 
-        def piece_closed(n):
-            if on(n - M2_LAG):
-                stage_f(n - M2_LAG)
-            if on(n - 1):
-                stage_d(n - 1)
-            j = n - M2_LAG - 1
-            if on(j):
-                stage_gq(j)
-                stage_stt(j)
-            if on(j - 1) and ends_batch(j - 1):
-                stage_ln2(links(j - 1)[0] // K)
-            if on(j) and ends_batch(j):
-                stage_ln1(links(j)[0] // K)
-            if on(n - 1):
-                stage_e(n - 1)
+        prepare_weights()
+        stage_a(0)
+        spread_rows()
+        stage_b(0)
+        for i in range(LAST_FULL + 1):
+            if i >= 1:
+                stage_d(i - 1, nc.vector.tensor_copy)
+                weave()
+            stage_a(i + 1)
+            if i >= 1:
+                stage_e(i - 1)
+            stage_c(i, 0)
+            stage_c(i, 1)
+            if i >= 1:
+                stage_f(i - 1)
+            stage_c(i, 2)
+            stage_c(i, 3)
+            stage_b(i + 1)
+            if i >= 1:
+                weave()
+                stage_g(i - 1)
+                weave()
+                stage_q(i - 1)
+                weave()
+                stage_stt(i - 1)
+                if ends_batch(i - 1):
+                    woven.extend(norm_ops(links(i - 1)[0] // K))
 
-        def h_bank(i):
-            n, t = divmod(i, 4)
-            stage_c(n, t)
-            if t == 3:
-                piece_closed(n)
-
-        with tc.manual_schedule():
-            for c in range(NCH):
-                stage_a(c, (0, 1, 2, 3))
-                if c == 0:
-                    prepare_weights()
-                if c == 1:
-                    spread_rows()
-                if c >= 1:
-                    stage_b(c - 1)
-                if c >= UNIT_LAG:
-                    h_bank(c - UNIT_LAG)
-            stage_b(NCH - 1)
-        for i in range(NCH - UNIT_LAG, 4 * NP):
-            h_bank(i)
-        for n in range(NP, NP + M2_LAG + 2):
-            piece_closed(n)
+        p, q = LAST_FULL + 1, LAST_FULL + 2
+        stage_d(LAST_FULL, nc.vector.tensor_copy)
+        for n in (p, q):
+            for t in range(4):
+                stage_c(n, t)
+        weave()
+        stage_e(LAST_FULL)
+        stage_f(LAST_FULL)
+        stage_d(p, nc.vector.tensor_copy)
+        stage_d(q, nc.scalar.copy)
+        weave()
+        stage_g(LAST_FULL)
+        stage_e(p)
+        stage_q(LAST_FULL)
+        weave()
+        stage_f(p)
+        stage_stt(LAST_FULL)
+        stage_g(p)
+        stage_e(q)
+        stage_q(p)
+        stage_f(q)
+        weave(len(woven))
+        stage_stt(p)
+        stage_g(q)
+        stage_q(q)
+        stage_stt(q)
+        for op in norm_ops(B - 1):
+            op()

@@ -37,8 +37,7 @@ def tile_embed_update_pa_t_kernel(tc, net_in, embeds, m, W1, b1, Wf, b_f, gamma,
         net = ctx.enter_context(tc.tile_pool(name="net", bufs=3))
         work = ctx.enter_context(tc.tile_pool(name="work", bufs=3))
         small = ctx.enter_context(tc.tile_pool(name="small", bufs=2))
-        tbanks = ctx.enter_context(tc.psum_pool(name="tbanks", bufs=4))
-        hbanks = ctx.enter_context(tc.psum_pool(name="hbanks", bufs=3))
+        banks = ctx.enter_context(tc.psum_pool(name="banks", bufs=7))
         obank = ctx.enter_context(tc.psum_pool(name="obank", bufs=1))
         ctx.enter_context(tc.manual_schedule())
 
@@ -149,7 +148,7 @@ def tile_embed_update_pa_t_kernel(tc, net_in, embeds, m, W1, b1, Wf, b_f, gamma,
             gnet[c] = gn
             for j in range(4):
                 lp, g = divmod(j, 2)
-                xt = tbanks.tile([P, 2, 2 * P], F32, name="xt", tag="bank")
+                xt = banks.tile([P, 2, 2 * P], F32, name="xt", tag="bank")
                 for u in range(2):
                     for li in range(2):
                         col = (2 * lp + li) * (IN // 2) + g * 256
@@ -172,7 +171,7 @@ def tile_embed_update_pa_t_kernel(tc, net_in, embeds, m, W1, b1, Wf, b_f, gamma,
                 hp_new = work.tile([P, 4, ROWS], BF16, name="hpl")
                 hpl[n] = hp_new
             rows = slice(l0 * P, (l0 + nl) * P)
-            hp = hbanks.tile([P, ROWS], F32, name="hp", tag="bank")
+            hp = banks.tile([P, ROWS], F32, name="hp", tag="bank")
             for g in range(2):
                 nc.tensor.matmul_mx(
                     out=hp[:, 0:nl * P],
@@ -211,7 +210,7 @@ def tile_embed_update_pa_t_kernel(tc, net_in, embeds, m, W1, b1, Wf, b_f, gamma,
 
         def stage_f(n):
             first, nl = links(n)
-            pool = obank if n <= LAST_FULL else tbanks
+            pool = obank if n <= LAST_FULL else banks
             op = pool.tile([P, LPC, CH], F32, name="op", tag="bank")
             opb[n] = op
             for l in range(nl):
@@ -327,48 +326,51 @@ def tile_embed_update_pa_t_kernel(tc, net_in, embeds, m, W1, b1, Wf, b_f, gamma,
         for i in range(LAST_FULL + 1):
             if i >= 1:
                 stage_d(i - 1, nc.vector.tensor_copy)
-                weave()
             stage_a(i + 1)
+            if i >= 2:
+                stage_g(i - 2)
             if i >= 1:
                 stage_e(i - 1)
-            stage_c(i, 0)
-            stage_c(i, 1)
+            if i >= 2 and i < LAST_FULL:
+                stage_q(i - 2)
+                weave()
+                stage_stt(i - 2)
+            for t in range(4):
+                stage_c(i, t)
             if i >= 1:
                 stage_f(i - 1)
-            stage_c(i, 2)
-            stage_c(i, 3)
             stage_b(i + 1)
-            if i >= 1:
+            if i == LAST_FULL:
+                stage_q(i - 2)
                 weave()
-                stage_g(i - 1)
-                weave()
-                stage_q(i - 1)
-                weave()
-                stage_stt(i - 1)
-                if ends_batch(i - 1):
-                    woven.extend(norm_ops(links(i - 1)[0] // K))
+                stage_stt(i - 2)
+            weave(2)
+            if i >= 2 and ends_batch(i - 2):
+                woven.extend(norm_ops(links(i - 2)[0] // K))
 
         p, q = LAST_FULL + 1, LAST_FULL + 2
         stage_d(LAST_FULL, nc.vector.tensor_copy)
+        stage_g(LAST_FULL - 1)
         for n in (p, q):
             for t in range(4):
                 stage_c(n, t)
-        weave()
         stage_e(LAST_FULL)
+        stage_q(LAST_FULL - 1)
         stage_f(LAST_FULL)
         stage_d(p, nc.vector.tensor_copy)
         stage_d(q, nc.scalar.copy)
-        weave()
-        stage_g(LAST_FULL)
+        stage_stt(LAST_FULL - 1)
         stage_e(p)
-        stage_q(LAST_FULL)
-        weave()
         stage_f(p)
+        stage_g(LAST_FULL)
+        weave()
+        stage_q(LAST_FULL)
+        stage_e(q)
+        stage_f(q)
         stage_stt(LAST_FULL)
         stage_g(p)
-        stage_e(q)
+        weave()
         stage_q(p)
-        stage_f(q)
         weave(len(woven))
         stage_stt(p)
         stage_g(q)

@@ -26,6 +26,7 @@ FLOPS = 2 * B * S * K * IN * HID + 2 * B * S * K * HID * CH
 PIECES = tuple((c, 0, LPC) for c in range(NCH - 1)) + ((NCH - 1, 0, 2), (NCH - 1, 2, 2))
 NP = len(PIECES)
 LAST_FULL = NCH - 2
+SORTED = 3
 
 
 def tile_embed_update_pa_t_kernel(tc, net_in, embeds, m, W1, b1, Wf, b_f, gamma, beta, out):
@@ -46,7 +47,7 @@ def tile_embed_update_pa_t_kernel(tc, net_in, embeds, m, W1, b1, Wf, b_f, gamma,
         def load(c):
             b, kq = divmod(c, K // LPC)
             xt_in = xpool.tile([P, LPC * IN], BF16, name="xin")
-            cuts = 2 if c == 0 else 1
+            cuts = 2 if c <= 1 else 1
             width = LPC * IN // cuts
             for h in range(cuts):
                 nc.sync.dma_start(
@@ -55,13 +56,13 @@ def tile_embed_update_pa_t_kernel(tc, net_in, embeds, m, W1, b1, Wf, b_f, gamma,
                 )
             xin[c] = xt_in
 
+        load(0)
         w1raw = const.tile([P, 8, HID], BF16)
         for g in range(2):
             nc.sync.dma_start(
                 out=w1raw[:, 4 * g:4 * g + 4, :].rearrange("p j h -> p (j h)"),
                 in_=W1[4 * P * g:4 * P * (g + 1), :].rearrange("(p j) h -> p (j h)", j=4),
             )
-        load(0)
         b1raw = const.tile([P, 4], BF16)
         nc.scalar.dma_start(out=b1raw[:], in_=b1.rearrange("(q t) -> q t", t=4))
         wfraw = const.tile([P, 4, CH], BF16)
@@ -125,44 +126,65 @@ def tile_embed_update_pa_t_kernel(tc, net_in, embeds, m, W1, b1, Wf, b_f, gamma,
                 in_=w1raw[:, 4 * g:4 * g + 4, :].rearrange("p j (q t) -> p t q j", t=4)[:, t0:t1],
             )
 
-        def prepare_weights():
-            regroup_w1(nc.vector.tensor_copy, 0, 0, 4)
-            regroup_w1(nc.scalar.copy, 1, 0, 2)
+        def prepare_small():
             nc.vector.tensor_copy(out=wfg[:], in_=wfraw[:].rearrange("p t c -> p c t"))
-            quantise_w1(0)
-            regroup_w1(nc.vector.tensor_copy, 1, 2, 4)
-            nc.vector.quantize_mx(out=wfc[:].bitcast(FP8X4), scales=wfs[:], in_=wfg[:].rearrange("p c t -> p (c t)"))
             nc.vector.tensor_copy(out=b1f[:], in_=b1raw[:])
+            nc.vector.quantize_mx(out=wfc[:].bitcast(FP8X4), scales=wfs[:], in_=wfg[:].rearrange("p c t -> p (c t)"))
             nc.vector.tensor_copy(out=mf[:], in_=msb[:].rearrange("p b k -> p (b k)"))
-            quantise_w1(1)
 
         sig = const.tile([P, B * K], F32)
         gall = const.tile([P, B * K], F32)
         sums_in = const.tile([P, B, 3, K], F32)
 
+        xsort = {}
         gnet, ncod, nsca, hpl, hgr, hcod, hsca, opb, acc = {}, {}, {}, {}, {}, {}, {}, {}, {}
 
-        def stage_a(c):
+        def sort_words(c):
+            lp, g = divmod(SORTED, 2)
+            xs = gpool.tile([P, 2, 2, P], F32, name="xsort")
+            xsort[c] = xs
+            words = xin[c][:].bitcast(F32).rearrange("p (l w) -> p l w", l=LPC)
+            nc.vector.tensor_copy(
+                out=xs[:],
+                in_=words[:, 2 * lp:2 * lp + 2, g * 2 * P:(g + 1) * 2 * P].rearrange("p l (m u) -> p l u m", u=2),
+            )
+
+        def stage_a(c, banks_of_c=(0, 1, 2, 3)):
             xf = xin[c][:].bitcast(F32)
-            gn = gpool.tile([P, 2, ROWS, 2], F32, name="gnet", align_bytes=64)
-            gnet[c] = gn
-            for j in range(4):
+            if c not in gnet:
+                gn_new = gpool.tile([P, 2, ROWS, 2], F32, name="gnet", align_bytes=64)
+                gnet[c] = gn_new
+            gn = gnet[c]
+            for j in banks_of_c:
                 lp, g = divmod(j, 2)
                 xt = banks.tile([P, 2, 2 * P], F32, name="xt", tag="bank")
                 for u in range(2):
                     for li in range(2):
                         col = (2 * lp + li) * (IN // 2) + g * 256
-                        nc.tensor.transpose(xt[:, u, li * P:(li + 1) * P], xf[:, col + u:col + 2 * P:2], ident[:])
+                        src = xsort[c][:, li, u, :] if j == SORTED and c in xsort else xf[:, col + u:col + 2 * P:2]
+                        nc.tensor.transpose(xt[:, u, li * P:(li + 1) * P], src, ident[:])
                 nc.scalar.copy(out=gn[:, g, lp * 2 * P:(lp + 1) * 2 * P, :], in_=xt[:].rearrange("p u r -> p r u"))
 
-        def stage_b(c):
+        def new_codes(c):
             nco = net.tile([P, 2, ROWS], U32, name="ncod", align_bytes=64)
             nsc = net.tile([P, 2, ROWS], U8, name="nsca", align_bytes=64)
             ncod[c], nsca[c] = nco, nsc
+
+        def stage_b(c):
+            new_codes(c)
             nc.vector.quantize_mx(
-                out=nco[:].rearrange("p g r -> p (g r)").bitcast(FP8X4),
-                scales=nsc[:].rearrange("p g r -> p (g r)"),
+                out=ncod[c][:].rearrange("p g r -> p (g r)").bitcast(FP8X4),
+                scales=nsca[c][:].rearrange("p g r -> p (g r)"),
                 in_=gnet[c][:].rearrange("p g r u -> p (g r u)").bitcast(BF16),
+            )
+
+        def stage_b_bank(c, j):
+            lp, g = divmod(j, 2)
+            rows = slice(lp * 2 * P, (lp + 1) * 2 * P)
+            nc.vector.quantize_mx(
+                out=ncod[c][:, g, rows].bitcast(FP8X4),
+                scales=nsca[c][:, g, rows],
+                in_=gnet[c][:, g, rows, :].rearrange("p r u -> p (r u)").bitcast(BF16),
             )
 
         def stage_c(n, t):
@@ -261,8 +283,8 @@ def tile_embed_update_pa_t_kernel(tc, net_in, embeds, m, W1, b1, Wf, b_f, gamma,
         woven = []
 
         def weave(count=1):
-            for op in woven[:count]:
-                op()
+            for step in woven[:count]:
+                step()
             woven[:count] = []
 
         def norm_ops(b):
@@ -295,61 +317,86 @@ def tile_embed_update_pa_t_kernel(tc, net_in, embeds, m, W1, b1, Wf, b_f, gamma,
                                                op0=ALU.mult, op1=ALU.add)
                 nc.sync.dma_start(out=out[b], in_=y2[:])
 
-            return [
-                lambda: nc.vector.tensor_scalar_add(out=sums_in[:, b, 0, :], in0=g16, scalar1=LINK_EPS),
-                lambda: nc.vector.scalar_tensor_tensor(out=sums_in[:, b, 1, :], in0=g16, scalar=LINK_EPS, in1=g16,
-                                                       op0=ALU.add, op1=ALU.mult),
-                lambda: nc.vector.tensor_reduce(out=sums[:], in_=sums_in[:, b], axis=AX.X, op=ALU.add),
-                lambda: nc.vector.reciprocal(out=rl[:], in_=sums[:, 0:1]),
-                lambda: nc.vector.scalar_tensor_tensor(out=w0[:], in0=bfb[:, 0:OUT], scalar=sums[:, 2:3],
-                                                       in1=a[:, 0, 0:OUT], op0=ALU.mult, op1=ALU.add),
-                lambda: nc.vector.tensor_scalar(out=s1[:], in0=sums[:, 1:2], scalar1=rl[:, 0:1], scalar2=rl[:, 0:1],
-                                                op0=ALU.mult, op1=ALU.mult),
-                lambda: nc.vector.tensor_tensor(out=w1[:], in0=w0[:], in1=a[:, 1, 0:OUT], op=ALU.add),
-                lambda: nc.vector.scalar_tensor_tensor(out=e2[:], in0=w1[:], scalar=s1[:, 0:1], in1=emb[:, b, 0:OUT],
-                                                       op0=ALU.mult, op1=ALU.add),
-                lambda: nc.vector.bn_stats(out=st6[:], in_=e2[:]),
-                variance,
-                lambda: nc.vector.scalar_tensor_tensor(out=y1[:], in0=e2[:], scalar=mv[:, 0:1], in1=gmb[:, 0:OUT],
-                                                       op0=ALU.subtract, op1=ALU.mult),
-                store,
-            ]
+            def link_weights():
+                nc.vector.tensor_scalar_add(out=sums_in[:, b, 0, :], in0=g16, scalar1=LINK_EPS)
+                nc.vector.scalar_tensor_tensor(out=sums_in[:, b, 1, :], in0=g16, scalar=LINK_EPS, in1=g16,
+                                               op0=ALU.add, op1=ALU.mult)
+
+            def link_sums():
+                nc.vector.tensor_reduce(out=sums[:], in_=sums_in[:, b], axis=AX.X, op=ALU.add)
+
+            def update_1():
+                nc.vector.reciprocal(out=rl[:], in_=sums[:, 0:1])
+                nc.vector.scalar_tensor_tensor(out=w0[:], in0=bfb[:, 0:OUT], scalar=sums[:, 2:3], in1=a[:, 0, 0:OUT],
+                                               op0=ALU.mult, op1=ALU.add)
+
+            def update_2():
+                nc.vector.tensor_scalar(out=s1[:], in0=sums[:, 1:2], scalar1=rl[:, 0:1], scalar2=rl[:, 0:1],
+                                        op0=ALU.mult, op1=ALU.mult)
+                nc.vector.tensor_tensor(out=w1[:], in0=w0[:], in1=a[:, 1, 0:OUT], op=ALU.add)
+
+            def update_3():
+                nc.vector.scalar_tensor_tensor(out=e2[:], in0=w1[:], scalar=s1[:, 0:1], in1=emb[:, b, 0:OUT],
+                                               op0=ALU.mult, op1=ALU.add)
+
+            def statistics():
+                nc.vector.bn_stats(out=st6[:], in_=e2[:])
+
+            def scaled():
+                nc.vector.scalar_tensor_tensor(out=y1[:], in0=e2[:], scalar=mv[:, 0:1], in1=gmb[:, 0:OUT],
+                                               op0=ALU.subtract, op1=ALU.mult)
+
+            return [link_weights, link_sums, update_1, update_2, update_3, statistics, variance, scaled, store]
 
         def ends_batch(n):
             first, nl = links(n)
             return (first + nl) % K == 0
 
-        prepare_weights()
-        stage_a(0)
+        prepare_small()
+        new_codes(0)
+        stage_a(0, (0, 1))
+        regroup_w1(nc.vector.tensor_copy, 0, 0, 4)
+        stage_b_bank(0, 0)
+        stage_b_bank(0, 1)
+        stage_a(0, (2, 3))
+        regroup_w1(nc.scalar.copy, 1, 0, 2)
+        regroup_w1(nc.vector.tensor_copy, 1, 2, 4)
+        stage_b_bank(0, 2)
+        stage_b_bank(0, 3)
+        quantise_w1(0)
+        quantise_w1(1)
         spread_rows()
-        stage_b(0)
         for i in range(LAST_FULL + 1):
             if i >= 1:
                 stage_d(i - 1, nc.vector.tensor_copy)
             stage_a(i + 1)
+            weave()
             if i >= 2:
                 stage_g(i - 2)
             if i >= 1:
                 stage_e(i - 1)
-            if i >= 2 and i < LAST_FULL:
+            if i >= 2:
                 stage_q(i - 2)
-                weave()
+            weave()
+            if i >= 2 and i < LAST_FULL:
                 stage_stt(i - 2)
+            weave()
+            if i + 2 < NCH:
+                sort_words(i + 2)
             for t in range(4):
                 stage_c(i, t)
             if i >= 1:
                 stage_f(i - 1)
             stage_b(i + 1)
             if i == LAST_FULL:
-                stage_q(i - 2)
-                weave()
                 stage_stt(i - 2)
-            weave(2)
+            weave()
             if i >= 2 and ends_batch(i - 2):
                 woven.extend(norm_ops(links(i - 2)[0] // K))
 
         p, q = LAST_FULL + 1, LAST_FULL + 2
         stage_d(LAST_FULL, nc.vector.tensor_copy)
+        weave()
         stage_g(LAST_FULL - 1)
         for n in (p, q):
             for t in range(4):

@@ -64,19 +64,22 @@ def tile_embed_update_pa_t_kernel(tc, net_in, embeds, m, W1, b1, Wf, b_f, gamma,
                 in_=W1[4 * P * g:4 * P * (g + 1), :].rearrange("(p j) h -> p (j h)", j=4),
             )
         b1raw = const.tile([P, 4], BF16)
-        nc.scalar.dma_start(out=b1raw[:], in_=b1.rearrange("(q t) -> q t", t=4))
+        nc.sync.dma_start(out=b1raw[:], in_=b1.rearrange("(q t) -> q t", t=4))
+        load(1)
         wfraw = const.tile([P, 4, CH], BF16)
-        nc.scalar.dma_start(out=wfraw[:].rearrange("p t c -> p (t c)"), in_=Wf.rearrange("(q t) c -> q (t c)", t=4))
+        nc.sync.dma_start(out=wfraw[:].rearrange("p t c -> p (t c)"), in_=Wf.rearrange("(q t) c -> q (t c)", t=4))
         rows3 = const.tile([P, 4, CH], BF16)
         nc.vector.memset(rows3[:], 0.0)
-        nc.scalar.dma_start(out=rows3[0:1, 0, :], in_=b_f.unsqueeze(0))
-        nc.scalar.dma_start(out=rows3[0:1, 1, 0:OUT], in_=gamma.unsqueeze(0))
-        nc.scalar.dma_start(out=rows3[0:1, 2, 0:OUT], in_=beta.unsqueeze(0))
+        nc.sync.dma_start(out=rows3[0:1, 0, :], in_=b_f.unsqueeze(0))
+        nc.sync.dma_start(out=rows3[0:1, 1, 0:OUT], in_=gamma.unsqueeze(0))
+        nc.sync.dma_start(out=rows3[0:1, 2, 0:OUT], in_=beta.unsqueeze(0))
+        load(2)
         msb = const.tile([P, B, K], BF16)
-        nc.scalar.dma_start(out=msb[:], in_=m.rearrange("b s k o -> s b (k o)"))
+        nc.sync.dma_start(out=msb[:], in_=m.rearrange("b s k o -> s b (k o)"))
+        load(3)
         emb = const.tile([P, B, CH], BF16)
-        nc.scalar.dma_start(out=emb[:, :, 0:OUT], in_=embeds.rearrange("b s c -> s b c"))
-        for c in range(1, NCH):
+        nc.sync.dma_start(out=emb[:, :, 0:OUT], in_=embeds.rearrange("b s c -> s b c"))
+        for c in range(4, NCH):
             load(c)
 
         junk = const.tile([P, 1], F32)
@@ -126,11 +129,10 @@ def tile_embed_update_pa_t_kernel(tc, net_in, embeds, m, W1, b1, Wf, b_f, gamma,
                 in_=w1raw[:, 4 * g:4 * g + 4, :].rearrange("p j (q t) -> p t q j", t=4)[:, t0:t1],
             )
 
-        def prepare_small():
+        def prepare_wf():
             nc.vector.tensor_copy(out=wfg[:], in_=wfraw[:].rearrange("p t c -> p c t"))
-            nc.vector.tensor_copy(out=b1f[:], in_=b1raw[:])
+            spread_rows()
             nc.vector.quantize_mx(out=wfc[:].bitcast(FP8X4), scales=wfs[:], in_=wfg[:].rearrange("p c t -> p (c t)"))
-            nc.vector.tensor_copy(out=mf[:], in_=msb[:].rearrange("p b k -> p (b k)"))
 
         sig = const.tile([P, B * K], F32)
         gall = const.tile([P, B * K], F32)
@@ -352,7 +354,6 @@ def tile_embed_update_pa_t_kernel(tc, net_in, embeds, m, W1, b1, Wf, b_f, gamma,
             first, nl = links(n)
             return (first + nl) % K == 0
 
-        prepare_small()
         new_codes(0)
         stage_a(0, (0, 1))
         regroup_w1(nc.vector.tensor_copy, 0, 0, 4)
@@ -364,29 +365,33 @@ def tile_embed_update_pa_t_kernel(tc, net_in, embeds, m, W1, b1, Wf, b_f, gamma,
         stage_b_bank(0, 2)
         stage_b_bank(0, 3)
         quantise_w1(0)
+        nc.vector.tensor_copy(out=b1f[:], in_=b1raw[:])
         quantise_w1(1)
-        spread_rows()
         for i in range(LAST_FULL + 1):
-            if i >= 1:
-                stage_d(i - 1, nc.vector.tensor_copy)
-            stage_a(i + 1)
-            weave()
             if i >= 2:
                 stage_g(i - 2)
             if i >= 1:
-                stage_e(i - 1)
+                stage_d(i - 1, nc.vector.tensor_copy)
+            stage_a(i + 1)
+            if i == 0:
+                prepare_wf()
+            if i == 1:
+                nc.vector.tensor_copy(out=mf[:], in_=msb[:].rearrange("p b k -> p (b k)"))
             if i >= 2:
                 stage_q(i - 2)
+            if i + 2 < NCH:
+                sort_words(i + 2)
+            weave()
+            if i >= 1:
+                stage_e(i - 1)
             weave()
             if i >= 2 and i < LAST_FULL:
                 stage_stt(i - 2)
-            weave()
-            if i + 2 < NCH:
-                sort_words(i + 2)
             for t in range(4):
                 stage_c(i, t)
             if i >= 1:
                 stage_f(i - 1)
+            weave()
             stage_b(i + 1)
             if i == LAST_FULL:
                 stage_stt(i - 2)
@@ -395,14 +400,14 @@ def tile_embed_update_pa_t_kernel(tc, net_in, embeds, m, W1, b1, Wf, b_f, gamma,
                 woven.extend(norm_ops(links(i - 2)[0] // K))
 
         p, q = LAST_FULL + 1, LAST_FULL + 2
-        stage_d(LAST_FULL, nc.vector.tensor_copy)
-        weave()
         stage_g(LAST_FULL - 1)
+        stage_d(LAST_FULL, nc.vector.tensor_copy)
+        stage_q(LAST_FULL - 1)
+        weave()
         for n in (p, q):
             for t in range(4):
                 stage_c(n, t)
         stage_e(LAST_FULL)
-        stage_q(LAST_FULL - 1)
         stage_f(LAST_FULL)
         stage_d(p, nc.vector.tensor_copy)
         stage_d(q, nc.scalar.copy)

@@ -234,7 +234,7 @@ def tile_embed_update_pa_t_kernel(tc, net_in, embeds, m, W1, b1, Wf, b_f, gamma,
 
         def stage_f(n):
             first, nl = links(n)
-            pool = obank if n <= LAST_FULL else banks
+            pool = obank if n < LAST_FULL else banks
             op = pool.tile([P, LPC, CH], F32, name="op", tag="bank")
             opb[n] = op
             for l in range(nl):
@@ -265,7 +265,7 @@ def tile_embed_update_pa_t_kernel(tc, net_in, embeds, m, W1, b1, Wf, b_f, gamma,
             nc.vector.scalar_tensor_tensor(out=sums_in[:, b, 2, k0:k0 + nl], in0=gall[:, cols], scalar=LINK_EPS,
                                            in1=mf[:, cols], op0=ALU.add, op1=ALU.mult)
 
-        def stage_stt(n):
+        def stage_stt(n, some=None):
             first, nl = links(n)
             b, k0 = divmod(first, K)
             op = opb[n]
@@ -273,7 +273,7 @@ def tile_embed_update_pa_t_kernel(tc, net_in, embeds, m, W1, b1, Wf, b_f, gamma,
                 acc_b = small.tile([P, 2, CH], F32, name="acc")
                 acc[b] = acc_b
             a = acc[b]
-            for l in range(nl):
+            for l in range(nl) if some is None else some:
                 k = k0 + l
                 qs = sums_in[:, b, 2, k:k + 1]
                 if k < 2:
@@ -321,6 +321,8 @@ def tile_embed_update_pa_t_kernel(tc, net_in, embeds, m, W1, b1, Wf, b_f, gamma,
 
             def link_weights():
                 nc.vector.tensor_scalar_add(out=sums_in[:, b, 0, :], in0=g16, scalar1=LINK_EPS)
+
+            def gate_products():
                 nc.vector.scalar_tensor_tensor(out=sums_in[:, b, 1, :], in0=g16, scalar=LINK_EPS, in1=g16,
                                                op0=ALU.add, op1=ALU.mult)
 
@@ -348,7 +350,16 @@ def tile_embed_update_pa_t_kernel(tc, net_in, embeds, m, W1, b1, Wf, b_f, gamma,
                 nc.vector.scalar_tensor_tensor(out=y1[:], in0=e2[:], scalar=mv[:, 0:1], in1=gmb[:, 0:OUT],
                                                op0=ALU.subtract, op1=ALU.mult)
 
-            return [link_weights, link_sums, update_1, update_2, update_3, statistics, variance, scaled, store]
+            return link_weights, gate_products, link_sums, [update_1, update_2, update_3, statistics, variance, scaled, store]
+
+        def norm_steps(b):
+            weights, products, sums, rest = norm_ops(b)
+
+            def both():
+                weights()
+                products()
+
+            return [both, sums] + rest
 
         def ends_batch(n):
             first, nl = links(n)
@@ -385,48 +396,54 @@ def tile_embed_update_pa_t_kernel(tc, net_in, embeds, m, W1, b1, Wf, b_f, gamma,
             if i >= 1:
                 stage_e(i - 1)
             weave()
-            if i >= 2 and i < LAST_FULL:
+            if i >= 2:
                 stage_stt(i - 2)
+                if ends_batch(i - 2):
+                    woven.extend(norm_steps(links(i - 2)[0] // K))
             for t in range(4):
                 stage_c(i, t)
             if i >= 1:
                 stage_f(i - 1)
             weave()
             stage_b(i + 1)
-            if i == LAST_FULL:
-                stage_stt(i - 2)
             weave()
-            if i >= 2 and ends_batch(i - 2):
-                woven.extend(norm_ops(links(i - 2)[0] // K))
 
         p, q = LAST_FULL + 1, LAST_FULL + 2
-        stage_g(LAST_FULL - 1)
-        stage_d(LAST_FULL, nc.vector.tensor_copy)
-        stage_q(LAST_FULL - 1)
-        weave()
         for n in (p, q):
             for t in range(4):
                 stage_c(n, t)
+        stage_d(LAST_FULL, nc.vector.tensor_copy)
+        stage_g(LAST_FULL - 1)
+        weave()
+        stage_q(LAST_FULL - 1)
         stage_e(LAST_FULL)
         stage_f(LAST_FULL)
-        stage_d(p, nc.vector.tensor_copy)
         stage_d(q, nc.scalar.copy)
-        stage_stt(LAST_FULL - 1)
+        stage_stt(LAST_FULL - 1, (0, 1))
+        stage_d(p, nc.vector.tensor_copy)
+        stage_stt(LAST_FULL - 1, (2, 3))
         stage_e(p)
         stage_f(p)
         stage_g(LAST_FULL)
-        weave()
+        weave(2)
         stage_q(LAST_FULL)
+        weave()
         stage_e(q)
         stage_f(q)
-        stage_stt(LAST_FULL)
         stage_g(p)
-        weave()
+        stage_stt(LAST_FULL, (0, 1))
         stage_q(p)
+        weave()
+        stage_stt(LAST_FULL, (2, 3))
         weave(len(woven))
         stage_stt(p)
+        weights, products, sums, rest = norm_ops(B - 1)
         stage_g(q)
+        weights()
         stage_q(q)
-        stage_stt(q)
-        for op in norm_ops(B - 1):
-            op()
+        products()
+        stage_stt(q, (0,))
+        sums()
+        stage_stt(q, (1,))
+        for step in rest:
+            step()

@@ -38,8 +38,8 @@ def tile_embed_update_pa_t_kernel(tc, net_in, embeds, m, W1, b1, Wf, b_f, gamma,
         net = ctx.enter_context(tc.tile_pool(name="net", bufs=3))
         work = ctx.enter_context(tc.tile_pool(name="work", bufs=3))
         small = ctx.enter_context(tc.tile_pool(name="small", bufs=2))
-        banks = ctx.enter_context(tc.psum_pool(name="banks", bufs=7))
-        obank = ctx.enter_context(tc.psum_pool(name="obank", bufs=1))
+        banks = ctx.enter_context(tc.psum_pool(name="banks", bufs=6))
+        obank = ctx.enter_context(tc.psum_pool(name="obank", bufs=2))
         ctx.enter_context(tc.manual_schedule())
 
         xin = {}

@@ -282,6 +282,7 @@ def tile_embed_update_pa_t_kernel(tc, net_in, embeds, m, W1, b1, Wf, b_f, gamma,
                     nc.vector.scalar_tensor_tensor(out=a[:, k % 2, :], in0=op[:, l, :], scalar=qs, in1=a[:, k % 2, :],
                                                    op0=ALU.mult, op1=ALU.add)
 
+        late = {}
         woven = []
 
         def weave(count=1):
@@ -307,12 +308,13 @@ def tile_embed_update_pa_t_kernel(tc, net_in, embeds, m, W1, b1, Wf, b_f, gamma,
 
             def variance():
                 nc.vector.bn_aggr(out=mv[:], in_=st6[:])
-                if b == B - 1:
-                    nc.scalar.activation(out=rstd[:], in_=mv[:, 1:2], func=ACT.Abs_reciprocal_sqrt,
-                                         bias=eps_ln[:, 0:1], scale=1.0)
-                else:
+                if b < B - 2:
                     nc.gpsimd.tensor_scalar_add(out=vpe[:], in0=mv[:, 1:2], scalar1=LN_EPS)
                     nc.gpsimd.tensor_tensor(out=rstd[:], in0=vpe[:], in1=neghalf[:], op=ALU.pow)
+
+            def scalar_rsqrt():
+                nc.scalar.activation(out=rstd[:], in_=mv[:, 1:2], func=ACT.Abs_reciprocal_sqrt,
+                                     bias=eps_ln[:, 0:1], scale=1.0)
 
             def store():
                 nc.vector.scalar_tensor_tensor(out=y2[:], in0=y1[:], scalar=rstd[:, 0:1], in1=btb[:, 0:OUT],
@@ -350,6 +352,8 @@ def tile_embed_update_pa_t_kernel(tc, net_in, embeds, m, W1, b1, Wf, b_f, gamma,
                 nc.vector.scalar_tensor_tensor(out=y1[:], in0=e2[:], scalar=mv[:, 0:1], in1=gmb[:, 0:OUT],
                                                op0=ALU.subtract, op1=ALU.mult)
 
+            if b >= B - 2:
+                late[b] = scalar_rsqrt, store
             return link_weights, gate_products, link_sums, [update_1, update_2, update_3, statistics, variance, scaled, store]
 
         def norm_steps(b):
@@ -359,7 +363,12 @@ def tile_embed_update_pa_t_kernel(tc, net_in, embeds, m, W1, b1, Wf, b_f, gamma,
                 weights()
                 products()
 
-            return [both, sums] + rest
+            def pause():
+                pass
+
+            if b == B - 2:
+                return [both, sums] + rest[:-1]
+            return [both, sums] + rest[:-1] + [pause, pause] + rest[-1:]
 
         def ends_batch(n):
             first, nl = links(n)
@@ -367,9 +376,9 @@ def tile_embed_update_pa_t_kernel(tc, net_in, embeds, m, W1, b1, Wf, b_f, gamma,
 
         new_codes(0)
         stage_a(0, (0, 1))
-        regroup_w1(nc.vector.tensor_copy, 0, 0, 4)
         stage_b_bank(0, 0)
         stage_b_bank(0, 1)
+        regroup_w1(nc.vector.tensor_copy, 0, 0, 4)
         stage_a(0, (2, 3))
         regroup_w1(nc.scalar.copy, 1, 0, 2)
         regroup_w1(nc.vector.tensor_copy, 1, 2, 4)
@@ -436,14 +445,25 @@ def tile_embed_update_pa_t_kernel(tc, net_in, embeds, m, W1, b1, Wf, b_f, gamma,
         weave()
         stage_stt(LAST_FULL, (2, 3))
         weave(len(woven))
-        stage_stt(p)
         weights, products, sums, rest = norm_ops(B - 1)
         stage_g(q)
+        stage_stt(p, (0,))
         weights()
         stage_q(q)
+        stage_stt(p, (1,))
         products()
         stage_stt(q, (0,))
         sums()
         stage_stt(q, (1,))
-        for step in rest:
-            step()
+        update_1, update_2, update_3, statistics, variance, scaled, store = rest
+        update_1()
+        update_2()
+        update_3()
+        before_rsqrt, before_store = late[B - 2]
+        before_rsqrt()
+        before_store()
+        statistics()
+        variance()
+        late[B - 1][0]()
+        scaled()
+        store()

@@ -26,7 +26,6 @@ FLOPS = 2 * B * S * K * IN * HID + 2 * B * S * K * HID * CH
 PIECES = tuple((c, 0, LPC) for c in range(NCH - 1)) + ((NCH - 1, 0, 2), (NCH - 1, 2, 2))
 NP = len(PIECES)
 LAST_FULL = NCH - 2
-SORTED = 3
 
 
 def tile_embed_update_pa_t_kernel(tc, net_in, embeds, m, W1, b1, Wf, b_f, gamma, beta, out):
@@ -38,6 +37,7 @@ def tile_embed_update_pa_t_kernel(tc, net_in, embeds, m, W1, b1, Wf, b_f, gamma,
         net = ctx.enter_context(tc.tile_pool(name="net", bufs=3))
         work = ctx.enter_context(tc.tile_pool(name="work", bufs=3))
         small = ctx.enter_context(tc.tile_pool(name="small", bufs=2))
+        late_pool = ctx.enter_context(tc.tile_pool(name="late_pool", bufs=B))
         banks = ctx.enter_context(tc.psum_pool(name="banks", bufs=6))
         obank = ctx.enter_context(tc.psum_pool(name="obank", bufs=2))
         ctx.enter_context(tc.manual_schedule())
@@ -88,8 +88,6 @@ def tile_embed_update_pa_t_kernel(tc, net_in, embeds, m, W1, b1, Wf, b_f, gamma,
 
         ident = const.tile([P, P], F32)
         make_identity(nc, ident[:])
-        neghalf = const.tile([P, 1], F32)
-        nc.vector.memset(neghalf[:], -0.5)
         ones = const.tile([P, P], BF16)
         nc.vector.memset(ones[:], 1.0)
         spread = const.tile([P, 3, CH], F32)
@@ -141,10 +139,10 @@ def tile_embed_update_pa_t_kernel(tc, net_in, embeds, m, W1, b1, Wf, b_f, gamma,
         xsort = {}
         gnet, ncod, nsca, hpl, hgr, hcod, hsca, opb, acc = {}, {}, {}, {}, {}, {}, {}, {}, {}
 
-        def sort_words(c):
-            lp, g = divmod(SORTED, 2)
+        def sort_words(c, j):
+            lp, g = divmod(j, 2)
             xs = gpool.tile([P, 2, 2, P], F32, name="xsort")
-            xsort[c] = xs
+            xsort[c, j] = xs
             words = xin[c][:].bitcast(F32).rearrange("p (l w) -> p l w", l=LPC)
             nc.vector.tensor_copy(
                 out=xs[:],
@@ -163,7 +161,7 @@ def tile_embed_update_pa_t_kernel(tc, net_in, embeds, m, W1, b1, Wf, b_f, gamma,
                 for u in range(2):
                     for li in range(2):
                         col = (2 * lp + li) * (IN // 2) + g * 256
-                        src = xsort[c][:, li, u, :] if j == SORTED and c in xsort else xf[:, col + u:col + 2 * P:2]
+                        src = xsort[c, j][:, li, u, :] if (c, j) in xsort else xf[:, col + u:col + 2 * P:2]
                         nc.tensor.transpose(xt[:, u, li * P:(li + 1) * P], src, ident[:])
                 nc.scalar.copy(out=gn[:, g, lp * 2 * P:(lp + 1) * 2 * P, :], in_=xt[:].rearrange("p u r -> p r u"))
 
@@ -299,18 +297,14 @@ def tile_embed_update_pa_t_kernel(tc, net_in, embeds, m, W1, b1, Wf, b_f, gamma,
             w1 = small.tile([P, OUT], F32, name="w1")
             e2 = small.tile([P, OUT], F32, name="e2")
             st6 = small.tile([P, 6], F32, name="st6")
-            mv = small.tile([P, 2], F32, name="mv")
-            vpe = small.tile([P, 1], F32, name="vpe")
-            rstd = small.tile([P, 1], F32, name="rstd")
-            y1 = small.tile([P, OUT], F32, name="y1")
-            y2 = small.tile([P, OUT], F32, name="y2")
+            mv = late_pool.tile([P, 2], F32, name="mv")
+            rstd = late_pool.tile([P, 1], F32, name="rstd")
+            y1 = late_pool.tile([P, OUT], F32, name="y1")
+            y2 = late_pool.tile([P, OUT], F32, name="y2")
             a = acc[b]
 
             def variance():
                 nc.vector.bn_aggr(out=mv[:], in_=st6[:])
-                if b < B - 2:
-                    nc.gpsimd.tensor_scalar_add(out=vpe[:], in0=mv[:, 1:2], scalar1=LN_EPS)
-                    nc.gpsimd.tensor_tensor(out=rstd[:], in0=vpe[:], in1=neghalf[:], op=ALU.pow)
 
             def scalar_rsqrt():
                 nc.scalar.activation(out=rstd[:], in_=mv[:, 1:2], func=ACT.Abs_reciprocal_sqrt,
@@ -352,8 +346,7 @@ def tile_embed_update_pa_t_kernel(tc, net_in, embeds, m, W1, b1, Wf, b_f, gamma,
                 nc.vector.scalar_tensor_tensor(out=y1[:], in0=e2[:], scalar=mv[:, 0:1], in1=gmb[:, 0:OUT],
                                                op0=ALU.subtract, op1=ALU.mult)
 
-            if b >= B - 2:
-                late[b] = scalar_rsqrt, store
+            late[b] = scalar_rsqrt, store
             return link_weights, gate_products, link_sums, [update_1, update_2, update_3, statistics, variance, scaled, store]
 
         def norm_steps(b):
@@ -363,12 +356,7 @@ def tile_embed_update_pa_t_kernel(tc, net_in, embeds, m, W1, b1, Wf, b_f, gamma,
                 weights()
                 products()
 
-            def pause():
-                pass
-
-            if b == B - 2:
-                return [both, sums] + rest[:-1]
-            return [both, sums] + rest[:-1] + [pause, pause] + rest[-1:]
+            return [both, sums] + rest[:-1]
 
         def ends_batch(n):
             first, nl = links(n)
@@ -400,7 +388,9 @@ def tile_embed_update_pa_t_kernel(tc, net_in, embeds, m, W1, b1, Wf, b_f, gamma,
             if i >= 2:
                 stage_q(i - 2)
             if i + 2 < NCH:
-                sort_words(i + 2)
+                sort_words(i + 2, 3)
+                if i < 3:
+                    sort_words(i + 2, 1)
             weave()
             if i >= 1:
                 stage_e(i - 1)
@@ -459,11 +449,13 @@ def tile_embed_update_pa_t_kernel(tc, net_in, embeds, m, W1, b1, Wf, b_f, gamma,
         update_1()
         update_2()
         update_3()
-        before_rsqrt, before_store = late[B - 2]
-        before_rsqrt()
-        before_store()
+        for b in range(B - 1):
+            late[b][0]()
+        late[0][1]()
         statistics()
+        late[1][1]()
         variance()
         late[B - 1][0]()
+        late[2][1]()
         scaled()
         store()

from contextlib import ExitStack

import concourse.mybir as mybir
from concourse.masks import make_identity

F32 = mybir.dt.float32
BF16 = mybir.dt.bfloat16
U32 = mybir.dt.uint32
U8 = mybir.dt.uint8
FP8X4 = mybir.dt.float8_e4m3fn_x4
ALU = mybir.AluOpType
ACT = mybir.ActivationFunctionType
AX = mybir.AxisListType

P = 128
B, S, K, IN, HID, OUT = 4, 128, 16, 1024, 512, 127
CH = OUT + 1
LPC = 4
NCH = B * K // LPC
ROWS = LPC * P
LN_EPS = 1e-5
LINK_EPS = 1e-8

FLOPS = 2 * B * S * K * IN * HID + 2 * B * S * K * HID * CH

PIECES = tuple((c, 0, LPC) for c in range(NCH - 1)) + ((NCH - 1, 0, 2), (NCH - 1, 2, 2))
NP = len(PIECES)
LAST_FULL = NCH - 2


def tile_embed_update_pa_t_kernel(tc, net_in, embeds, m, W1, b1, Wf, b_f, gamma, beta, out):
    nc = tc.nc
    with ExitStack() as ctx:
        const = ctx.enter_context(tc.tile_pool(name="const", bufs=1))
        xpool = ctx.enter_context(tc.tile_pool(name="xpool", bufs=6))
        gpool = ctx.enter_context(tc.tile_pool(name="gpool", bufs=3))
        net = ctx.enter_context(tc.tile_pool(name="net", bufs=3))
        work = ctx.enter_context(tc.tile_pool(name="work", bufs=3))
        small = ctx.enter_context(tc.tile_pool(name="small", bufs=2))
        late_pool = ctx.enter_context(tc.tile_pool(name="late_pool", bufs=B))
        banks = ctx.enter_context(tc.psum_pool(name="banks", bufs=6))
        obank = ctx.enter_context(tc.psum_pool(name="obank", bufs=2))
        ctx.enter_context(tc.manual_schedule())

        xin = {}

        def load(c):
            b, kq = divmod(c, K // LPC)
            xt_in = xpool.tile([P, LPC * IN], BF16, name="xin")
            cuts = 2 if c <= 1 else 1
            width = LPC * IN // cuts
            for h in range(cuts):
                nc.sync.dma_start(
                    out=xt_in[:, h * width:(h + 1) * width],
                    in_=net_in[b].rearrange("s k i -> s (k i)")[:, kq * LPC * IN + h * width:kq * LPC * IN + (h + 1) * width],
                )
            xin[c] = xt_in

        load(0)
        w1raw = const.tile([P, 8, HID], BF16)
        for g in range(2):
            nc.sync.dma_start(
                out=w1raw[:, 4 * g:4 * g + 4, :].rearrange("p j h -> p (j h)"),
                in_=W1[4 * P * g:4 * P * (g + 1), :].rearrange("(p j) h -> p (j h)", j=4),
            )
        b1raw = const.tile([P, 4], BF16)
        nc.sync.dma_start(out=b1raw[:], in_=b1.rearrange("(q t) -> q t", t=4))
        load(1)
        wfraw = const.tile([P, 4, CH], BF16)
        nc.sync.dma_start(out=wfraw[:].rearrange("p t c -> p (t c)"), in_=Wf.rearrange("(q t) c -> q (t c)", t=4))
        rows3 = const.tile([P, 4, CH], BF16)
        nc.vector.memset(rows3[:], 0.0)
        nc.sync.dma_start(out=rows3[0:1, 0, :], in_=b_f.unsqueeze(0))
        nc.sync.dma_start(out=rows3[0:1, 1, 0:OUT], in_=gamma.unsqueeze(0))
        nc.sync.dma_start(out=rows3[0:1, 2, 0:OUT], in_=beta.unsqueeze(0))
        load(2)
        msb = const.tile([P, B, K], BF16)
        nc.sync.dma_start(out=msb[:], in_=m.rearrange("b s k o -> s b (k o)"))
        load(3)
        emb = const.tile([P, B, CH], BF16)
        nc.sync.dma_start(out=emb[:, :, 0:OUT], in_=embeds.rearrange("b s c -> s b c"))
        for c in range(4, NCH):
            load(c)

        junk = const.tile([P, 1], F32)
        nc.vector.memset(junk[:], 0.0)
        nc.scalar.activation(out=junk[:], in_=junk[:], func=ACT.Sigmoid)

        ident = const.tile([P, P], F32)
        make_identity(nc, ident[:])
        ones = const.tile([P, P], BF16)
        nc.vector.memset(ones[:], 1.0)
        spread = const.tile([P, 3, CH], F32)
        eps_ln = const.tile([P, 1], F32)
        nc.vector.memset(eps_ln[:], LN_EPS)

        def spread_rows():
            spread_ps = obank.tile([P, LPC, CH], F32, name="spread_ps", tag="bank")
            nc.tensor.matmul(out=spread_ps[:], lhsT=ones[:], rhs=rows3[:], start=True, stop=True)
            nc.vector.tensor_copy(out=spread[:], in_=spread_ps[:, 0:3, :])
            nc.vector.tensor_copy(out=bf127[:], in_=bfb[:, OUT:CH])

        bfb = spread[:, 0, :]
        gmb = spread[:, 1, :]
        btb = spread[:, 2, :]

        w1g = const.tile([P, 2, HID, 4], BF16, align_bytes=64)
        w1c = const.tile([P, 2, HID], U32, align_bytes=64)
        w1s = const.tile([P, 2, HID], U8, align_bytes=64)
        b1f = const.tile([P, 4], F32)
        wfg = const.tile([P, CH, 4], BF16, align_bytes=64)
        bf127 = const.tile([P, 1], F32)
        mf = const.tile([P, B * K], F32)
        wfc = const.tile([P, CH], U32, align_bytes=64)
        wfs = const.tile([P, CH], U8, align_bytes=64)

        def quantise_w1(g):
            nc.vector.quantize_mx(
                out=w1c[:, g, :].bitcast(FP8X4),
                scales=w1s[:, g, :],
                in_=w1g[:, g].rearrange("p h j -> p (h j)"),
            )

        def regroup_w1(copy, g, t0, t1):
            copy(
                out=w1g[:, g].rearrange("p (t q) j -> p t q j", t=4)[:, t0:t1],
                in_=w1raw[:, 4 * g:4 * g + 4, :].rearrange("p j (q t) -> p t q j", t=4)[:, t0:t1],
            )

        def prepare_wf():
            nc.vector.tensor_copy(out=wfg[:], in_=wfraw[:].rearrange("p t c -> p c t"))
            spread_rows()
            nc.vector.quantize_mx(out=wfc[:].bitcast(FP8X4), scales=wfs[:], in_=wfg[:].rearrange("p c t -> p (c t)"))

        sig = const.tile([P, B * K], F32)
        gall = const.tile([P, B * K], F32)
        sums_in = const.tile([P, B, 3, K], F32)

        xsort = {}
        gnet, ncod, nsca, hpl, hgr, hcod, hsca, opb, acc = {}, {}, {}, {}, {}, {}, {}, {}, {}

        def sort_words(c, j):
            lp, g = divmod(j, 2)
            xs = gpool.tile([P, 2, 2, P], F32, name="xsort")
            xsort[c, j] = xs
            words = xin[c][:].bitcast(F32).rearrange("p (l w) -> p l w", l=LPC)
            nc.vector.tensor_copy(
                out=xs[:],
                in_=words[:, 2 * lp:2 * lp + 2, g * 2 * P:(g + 1) * 2 * P].rearrange("p l (m u) -> p l u m", u=2),
            )

        def stage_a(c, banks_of_c=(0, 1, 2, 3)):
            xf = xin[c][:].bitcast(F32)
            if c not in gnet:
                gn_new = gpool.tile([P, 2, ROWS, 2], F32, name="gnet", align_bytes=64)
                gnet[c] = gn_new
            gn = gnet[c]
            for j in banks_of_c:
                lp, g = divmod(j, 2)
                xt = banks.tile([P, 2, 2 * P], F32, name="xt", tag="bank")
                for u in range(2):
                    for li in range(2):
                        col = (2 * lp + li) * (IN // 2) + g * 256
                        src = xsort[c, j][:, li, u, :] if (c, j) in xsort else xf[:, col + u:col + 2 * P:2]
                        nc.tensor.transpose(xt[:, u, li * P:(li + 1) * P], src, ident[:])
                nc.scalar.copy(out=gn[:, g, lp * 2 * P:(lp + 1) * 2 * P, :], in_=xt[:].rearrange("p u r -> p r u"))

        def new_codes(c):
            nco = net.tile([P, 2, ROWS], U32, name="ncod", align_bytes=64)
            nsc = net.tile([P, 2, ROWS], U8, name="nsca", align_bytes=64)
            ncod[c], nsca[c] = nco, nsc

        def stage_b(c):
            new_codes(c)
            nc.vector.quantize_mx(
                out=ncod[c][:].rearrange("p g r -> p (g r)").bitcast(FP8X4),
                scales=nsca[c][:].rearrange("p g r -> p (g r)"),
                in_=gnet[c][:].rearrange("p g r u -> p (g r u)").bitcast(BF16),
            )

        def stage_b_bank(c, j):
            lp, g = divmod(j, 2)
            rows = slice(lp * 2 * P, (lp + 1) * 2 * P)
            nc.vector.quantize_mx(
                out=ncod[c][:, g, rows].bitcast(FP8X4),
                scales=nsca[c][:, g, rows],
                in_=gnet[c][:, g, rows, :].rearrange("p r u -> p (r u)").bitcast(BF16),
            )

        def stage_c(n, t):
            c, l0, nl = PIECES[n]
            if n not in hpl:
                hp_new = work.tile([P, 4, ROWS], BF16, name="hpl")
                hpl[n] = hp_new
            rows = slice(l0 * P, (l0 + nl) * P)
            hp = banks.tile([P, ROWS], F32, name="hp", tag="bank")
            for g in range(2):
                nc.tensor.matmul_mx(
                    out=hp[:, 0:nl * P],
                    lhsT=w1c[:, g, t * P:(t + 1) * P].bitcast(FP8X4),
                    lhsT_scale=w1s[:, g, t * P:(t + 1) * P],
                    rhs=ncod[c][:, g, rows].bitcast(FP8X4),
                    rhs_scale=nsca[c][:, g, rows],
                    start=(g == 0),
                    stop=(g == 1),
                )
            nc.scalar.activation(out=hpl[n][:, t, 0:nl * P], in_=hp[:, 0:nl * P], func=ACT.Relu,
                                 bias=b1f[:, t:t + 1], scale=1.0)

        def regroup(copy, n, r0, r1):
            copy(
                out=hgr[n][:, r0:r1, :].rearrange("p (c i) t -> p c t i", i=4),
                in_=hpl[n][:, :, r0:r1].rearrange("p t (c i) -> p c t i", i=4),
            )

        def stage_d(n, copy):
            hg = work.tile([P, ROWS, 4], BF16, name="hgr", align_bytes=64)
            hgr[n] = hg
            regroup(copy, n, 0, PIECES[n][2] * P)

        def stage_e(n):
            nl = PIECES[n][2]
            hco = work.tile([P, ROWS], U32, name="hcod", align_bytes=64)
            hsc = work.tile([P, ROWS], U8, name="hsca", align_bytes=64)
            hcod[n], hsca[n] = hco, hsc
            nc.vector.quantize_mx(out=hco[:, 0:nl * P].bitcast(FP8X4), scales=hsc[:, 0:nl * P],
                                  in_=hgr[n][:, 0:nl * P, :].rearrange("p r t -> p (r t)"))

        def links(n):
            c, l0, nl = PIECES[n]
            return c * LPC + l0, nl

        def stage_f(n):
            first, nl = links(n)
            pool = obank if n < LAST_FULL else banks
            op = pool.tile([P, LPC, CH], F32, name="op", tag="bank")
            opb[n] = op
            for l in range(nl):
                nc.tensor.matmul_mx(
                    out=op[:, l, :],
                    lhsT=hcod[n][:, l * P:(l + 1) * P].bitcast(FP8X4),
                    lhsT_scale=hsca[n][:, l * P:(l + 1) * P],
                    rhs=wfc[:].bitcast(FP8X4),
                    rhs_scale=wfs[:],
                    start=True,
                    stop=True,
                )
            nc.scalar.activation(out=sig[:, first:first + nl], in_=op[:, 0:nl, OUT], func=ACT.Sigmoid,
                                 bias=bf127[:, 0:1], scale=1.0)
            if n == NP - 1:
                nc.scalar.activation(out=junk[:], in_=sig[:, first:first + 1], func=ACT.Abs_reciprocal_sqrt,
                                     bias=eps_ln[:, 0:1], scale=1.0)

        def stage_g(n):
            first, nl = links(n)
            cols = slice(first, first + nl)
            nc.vector.tensor_tensor(out=gall[:, cols], in0=sig[:, cols], in1=mf[:, cols], op=ALU.mult)

        def stage_q(n):
            first, nl = links(n)
            b, k0 = divmod(first, K)
            cols = slice(first, first + nl)
            nc.vector.scalar_tensor_tensor(out=sums_in[:, b, 2, k0:k0 + nl], in0=gall[:, cols], scalar=LINK_EPS,
                                           in1=mf[:, cols], op0=ALU.add, op1=ALU.mult)

        def stage_stt(n, some=None):
            first, nl = links(n)
            b, k0 = divmod(first, K)
            op = opb[n]
            if k0 == 0:
                acc_b = small.tile([P, 2, CH], F32, name="acc")
                acc[b] = acc_b
            a = acc[b]
            for l in range(nl) if some is None else some:
                k = k0 + l
                qs = sums_in[:, b, 2, k:k + 1]
                if k < 2:
                    nc.vector.tensor_scalar(out=a[:, k % 2, :], in0=op[:, l, :], scalar1=qs, scalar2=None, op0=ALU.mult)
                else:
                    nc.vector.scalar_tensor_tensor(out=a[:, k % 2, :], in0=op[:, l, :], scalar=qs, in1=a[:, k % 2, :],
                                                   op0=ALU.mult, op1=ALU.add)

        late = {}
        woven = []

        def weave(count=1):
            for step in woven[:count]:
                step()
            woven[:count] = []

        def norm_ops(b):
            g16 = gall[:, b * K:(b + 1) * K]
            sums = small.tile([P, 3], F32, name="sums")
            rl = small.tile([P, 1], F32, name="rl")
            s1 = small.tile([P, 1], F32, name="s1")
            w0 = small.tile([P, OUT], F32, name="w0")
            w1 = small.tile([P, OUT], F32, name="w1")
            e2 = small.tile([P, OUT], F32, name="e2")
            st6 = small.tile([P, 6], F32, name="st6")
            mv = late_pool.tile([P, 2], F32, name="mv")
            rstd = late_pool.tile([P, 1], F32, name="rstd")
            y1 = late_pool.tile([P, OUT], F32, name="y1")
            y2 = late_pool.tile([P, OUT], F32, name="y2")
            a = acc[b]

            def variance():
                nc.vector.bn_aggr(out=mv[:], in_=st6[:])

            def scalar_rsqrt():
                nc.scalar.activation(out=rstd[:], in_=mv[:, 1:2], func=ACT.Abs_reciprocal_sqrt,
                                     bias=eps_ln[:, 0:1], scale=1.0)

            def store():
                nc.vector.scalar_tensor_tensor(out=y2[:], in0=y1[:], scalar=rstd[:, 0:1], in1=btb[:, 0:OUT],
                                               op0=ALU.mult, op1=ALU.add)
                nc.sync.dma_start(out=out[b], in_=y2[:])

            def link_weights():
                nc.vector.tensor_scalar_add(out=sums_in[:, b, 0, :], in0=g16, scalar1=LINK_EPS)

            def gate_products():
                nc.vector.scalar_tensor_tensor(out=sums_in[:, b, 1, :], in0=g16, scalar=LINK_EPS, in1=g16,
                                               op0=ALU.add, op1=ALU.mult)

            def link_sums():
                nc.vector.tensor_reduce(out=sums[:], in_=sums_in[:, b], axis=AX.X, op=ALU.add)

            def update_1():
                nc.vector.reciprocal(out=rl[:], in_=sums[:, 0:1])
                nc.vector.scalar_tensor_tensor(out=w0[:], in0=bfb[:, 0:OUT], scalar=sums[:, 2:3], in1=a[:, 0, 0:OUT],
                                               op0=ALU.mult, op1=ALU.add)

            def update_2():
                nc.vector.tensor_scalar(out=s1[:], in0=sums[:, 1:2], scalar1=rl[:, 0:1], scalar2=rl[:, 0:1],
                                        op0=ALU.mult, op1=ALU.mult)
                nc.vector.tensor_tensor(out=w1[:], in0=w0[:], in1=a[:, 1, 0:OUT], op=ALU.add)

            def update_3():
                nc.vector.scalar_tensor_tensor(out=e2[:], in0=w1[:], scalar=s1[:, 0:1], in1=emb[:, b, 0:OUT],
                                               op0=ALU.mult, op1=ALU.add)

            def statistics():
                nc.vector.bn_stats(out=st6[:], in_=e2[:])

            def scaled():
                nc.vector.scalar_tensor_tensor(out=y1[:], in0=e2[:], scalar=mv[:, 0:1], in1=gmb[:, 0:OUT],
                                               op0=ALU.subtract, op1=ALU.mult)

            late[b] = scalar_rsqrt, store
            return link_weights, gate_products, link_sums, [update_1, update_2, update_3, statistics, variance, scaled, store]

        def norm_steps(b):
            weights, products, sums, rest = norm_ops(b)

            def both():
                weights()
                products()

            return [both, sums] + rest[:-1]

        def ends_batch(n):
            first, nl = links(n)
            return (first + nl) % K == 0

        new_codes(0)
        stage_a(0, (0, 1))
        stage_b_bank(0, 0)
        stage_b_bank(0, 1)
        regroup_w1(nc.vector.tensor_copy, 0, 0, 4)
        stage_a(0, (2, 3))
        regroup_w1(nc.scalar.copy, 1, 0, 2)
        regroup_w1(nc.vector.tensor_copy, 1, 2, 4)
        stage_b_bank(0, 2)
        stage_b_bank(0, 3)
        quantise_w1(0)
        nc.vector.tensor_copy(out=b1f[:], in_=b1raw[:])
        quantise_w1(1)
        for i in range(LAST_FULL + 1):
            if i >= 2:
                stage_g(i - 2)
            if i >= 1:
                stage_d(i - 1, nc.vector.tensor_copy)
            stage_a(i + 1)
            if i == 0:
                prepare_wf()
            if i == 1:
                nc.vector.tensor_copy(out=mf[:], in_=msb[:].rearrange("p b k -> p (b k)"))
            if i >= 2:
                stage_q(i - 2)
            if i + 2 < NCH:
                sort_words(i + 2, 3)
                if i < 3:
                    sort_words(i + 2, 1)
            weave()
            if i >= 1:
                stage_e(i - 1)
            weave()
            if i >= 2:
                stage_stt(i - 2)
                if ends_batch(i - 2):
                    woven.extend(norm_steps(links(i - 2)[0] // K))
            for t in range(4):
                stage_c(i, t)
            if i >= 1:
                stage_f(i - 1)
            weave()
            stage_b(i + 1)
            weave()

        p, q = LAST_FULL + 1, LAST_FULL + 2
        for n in (p, q):
            for t in range(4):
                stage_c(n, t)
        stage_d(LAST_FULL, nc.vector.tensor_copy)
        stage_g(LAST_FULL - 1)
        weave()
        stage_q(LAST_FULL - 1)
        stage_e(LAST_FULL)
        stage_f(LAST_FULL)
        stage_d(q, nc.scalar.copy)
        stage_stt(LAST_FULL - 1, (0, 1))
        stage_d(p, nc.vector.tensor_copy)
        stage_stt(LAST_FULL - 1, (2, 3))
        stage_e(p)
        stage_f(p)
        stage_g(LAST_FULL)
        weave(2)
        stage_q(LAST_FULL)
        weave()
        stage_e(q)
        stage_f(q)
        stage_g(p)
        stage_stt(LAST_FULL, (0, 1))
        stage_q(p)
        weave()
        stage_stt(LAST_FULL, (2, 3))
        weave(len(woven))
        weights, products, sums, rest = norm_ops(B - 1)
        stage_g(q)
        stage_stt(p, (0,))
        weights()
        stage_q(q)
        stage_stt(p, (1,))
        products()
        stage_stt(q, (0,))
        sums()
        stage_stt(q, (1,))
        update_1, update_2, update_3, statistics, variance, scaled, store = rest
        update_1()
        update_2()
        update_3()
        for b in range(B - 1):
            late[b][0]()
        late[0][1]()
        statistics()
        late[1][1]()
        variance()
        late[B - 1][0]()
        late[2][1]()
        scaled()
        store()
